import numpy as np
import ml_dtypes


def mxq(x, axis, fmt="e4m3"):
    dtype, down = {"e4m3": (ml_dtypes.float8_e4m3fn, 7), "e5m2": (ml_dtypes.float8_e5m2, 14)}[fmt]
    v = np.moveaxis(np.asarray(x, np.float32).astype(ml_dtypes.bfloat16).astype(np.float64), axis, -1)
    blocks = v.reshape(v.shape[:-1] + (-1, 32))
    amax = np.abs(blocks).max(-1, keepdims=True)
    byte = np.maximum(np.where(amax > 0, np.frexp(amax)[1] - 1 + 127, 0) - down, 1)
    scale = np.exp2(byte - 127.0)
    codes = (blocks / scale).astype(np.float32).astype(dtype).astype(np.float64)
    return np.moveaxis((codes * scale).reshape(v.shape), -1, axis)


WIDE = False


def mx_kscale(k):
    if not WIDE:
        return np.ones(k)
    levels = np.array([10, -10, 5, -5, 0])
    a = np.random.permutation(np.resize(levels, k // 512 * 4)).reshape(k // 512, 4)
    idx = np.arange(k)
    return np.exp2(a[idx // 512, idx % 128 // 32])


BF16 = ml_dtypes.bfloat16


def bf(x):
    return np.asarray(x, np.float32).astype(BF16)


def f64(x):
    return np.asarray(x).astype(np.float64)


E2M1 = np.array([0.0, 0.5, 1.0, 1.5, 2.0, 3.0, 4.0, 6.0, -0.0, -0.5, -1.0, -1.5, -2.0, -3.0, -4.0, -6.0])


def pack_weight(w, fmt):
    k, n = w.shape
    w = f64(bf(w)).reshape(k // 32, 32, n)
    amax = np.abs(w).max(1)
    if fmt == "e4m3":
        byte = np.frexp(amax)[1] - 1 + 127 - 7
    else:
        mant, ex = np.frexp(amax / 6.0)
        byte = np.where(mant > 0.5, ex, ex - 1) + 127
    byte = np.clip(np.where(amax > 0, byte, 1), 1, 254)
    scaled = (w * np.exp2(127.0 - byte)[:, None, :]).reshape(k, n).astype(np.float32)
    by_word = np.ascontiguousarray(scaled.reshape(k // 512, 128, 4, n).transpose(0, 1, 3, 2))
    if fmt == "e4m3":
        words = by_word.astype(ml_dtypes.float8_e4m3fn).view(np.uint8)
    else:
        c = by_word.astype(ml_dtypes.float4_e2m1fn).view(np.uint8) & 0xF
        words = c[..., 0::2] | (c[..., 1::2] << 4)
    return np.ascontiguousarray(words), np.ascontiguousarray(byte.astype(np.uint8).reshape(k // 512, 16, n))


def unpack_weight(words, scales, fmt):
    g, p, n, _ = words.shape
    if fmt == "e4m3":
        vals = np.ascontiguousarray(words).view(ml_dtypes.float8_e4m3fn).astype(np.float64)
    else:
        nib = np.empty((g, p, n, 4), np.uint8)
        nib[..., 0::2] = words & 0xF
        nib[..., 1::2] = words >> 4
        vals = E2M1[nib]
    vals = vals * np.repeat(np.exp2(scales.astype(np.float64) - 127.0), 8, axis=1)[..., None]
    return vals.transpose(0, 1, 3, 2).reshape(g * 512, n)


B, IN_F, FEAT, NCLASS = 1024, 1024, 512, 1024
D = 4 * FEAT
GAMMA = 0.1
FMT = "e4m3"


def setup_inputs():
    s = mx_kscale(IN_F)
    ws = 0.5 / np.sqrt(IN_F)
    x = bf(np.random.standard_normal((B, IN_F)) * s)
    x_90 = bf(np.random.standard_normal((B, IN_F)) * s)
    x_180 = bf(np.random.standard_normal((B, IN_F)) * s)
    x_270 = bf(np.random.standard_normal((B, IN_F)) * s)
    wf_words, wf_scales = pack_weight((np.random.standard_normal((FEAT, IN_F)) * ws / s).T, FMT)
    b_f = bf(np.random.standard_normal(FEAT) * 0.25)
    wr_words, wr_scales = pack_weight((np.random.standard_normal((FEAT, IN_F)) * ws / s).T, FMT)
    b_r = bf(np.random.standard_normal(FEAT) * 0.25)
    centers = bf(0.2 + 0.3 * np.random.standard_normal((NCLASS, D)))
    return {
        "x": x,
        "x_90": x_90,
        "x_180": x_180,
        "x_270": x_270,
        "W_f_words": wf_words,
        "W_f_scales": wf_scales,
        "b_f": b_f,
        "W_r_words": wr_words,
        "W_r_scales": wr_scales,
        "b_r": b_r,
        "centers": centers,
    }


def reference(x, x_90, x_180, x_270, W_f_words, W_f_scales, b_f, W_r_words, W_r_scales, b_r, centers):
    wf = unpack_weight(W_f_words, W_f_scales, FMT).T
    wr = unpack_weight(W_r_words, W_r_scales, FMT).T
    f = np.maximum((mxq(f64(x), 1, "e4m3") @ wf.T) + f64(b_f), 0.0)
    f90 = np.maximum((mxq(f64(x_90), 1, "e4m3") @ wr.T) + f64(b_r), 0.0)
    f180 = np.maximum((mxq(f64(x_180), 1, "e4m3") @ wr.T) + f64(b_r), 0.0)
    f270 = np.maximum((mxq(f64(x_270), 1, "e4m3") @ wr.T) + f64(b_r), 0.0)
    feat = np.concatenate((f, f90, f180, f270), axis=1)
    c = f64(centers)
    f2 = np.sum(feat * feat, axis=1, keepdims=True)
    c2 = np.sum(c * c, axis=1)
    d2 = f2 + c2[None, :] - 2.0 * (mxq(feat, 1, "e4m3") @ mxq(c, 1, "e4m3").T)
    return np.sqrt(np.maximum(d2, 0.0)) * (-GAMMA)

@@ -1,0 +1,293 @@
+from contextlib import ExitStack
+
+import concourse.mybir as mybir
+from concourse.masks import make_identity
+
+F32 = mybir.dt.float32
+BF16 = mybir.dt.bfloat16
+I32 = mybir.dt.int32
+U32 = mybir.dt.uint32
+U8 = mybir.dt.uint8
+FP8X4 = mybir.dt.float8_e4m3fn_x4
+ACT = mybir.ActivationFunctionType
+ALU = mybir.AluOpType
+
+P = 128
+PACK = 4
+K_PASS = P * PACK
+BANK = 512
+
+BATCH, IN_F, FEAT, NCLASS = 1024, 1024, 512, 1024
+VIEWS = 4
+D = VIEWS * FEAT
+GAMMA = 0.1
+
+HALVES = BATCH // BANK
+ROW_TILES = BANK // P
+IN_PASSES = IN_F // K_PASS
+UNITS = HALVES * VIEWS
+CENTRE_HALVES = NCLASS // BANK
+CENTRE_BLOCKS = CENTRE_HALVES * VIEWS
+BLOCKS_PER_STEP = 2
+PROJECT_LAG = 1
+NORM_LAG = 2
+
+FLOPS = 2 * BATCH * IN_F * FEAT * VIEWS + 2 * BATCH * D * NCLASS
+
+
+def tile_qccpn_pa_kernel(
+    tc, x, x_90, x_180, x_270, W_f_words, W_f_scales, b_f, W_r_words, W_r_scales, b_r, centers, out
+):
+    nc = tc.nc
+    views = [x, x_90, x_180, x_270]
+    weight_of_view = [0, 1, 1, 1]
+    units = [(h, v) for h in range(HALVES) for v in range(VIEWS)]
+
+    with ExitStack() as stack:
+        keep = stack.enter_context(tc.tile_pool(name="keep", bufs=1))
+        stream = stack.enter_context(tc.tile_pool(name="stream", bufs=2))
+        psum = stack.enter_context(tc.psum_pool(name="psum", bufs=2))
+
+        def load_unit(h, v):
+            x_raw = stream.tile([P, ROW_TILES, IN_F], BF16, tag="x_raw", bufs=4)
+            rows = views[v].rearrange("(h p j) k -> h p j k", h=HALVES, p=P)
+            nc.sync.dma_start(out=x_raw[:], in_=rows[h])
+            return x_raw
+
+        def load_centre_half(ch):
+            c_raw = stream.tile([P, ROW_TILES, D], BF16, tag="c_raw", bufs=CENTRE_HALVES)
+            rows = centers.rearrange("(ch i p) k -> ch i p k", ch=CENTRE_HALVES, p=P)
+            for i in range(ROW_TILES):
+                nc.sync.dma_start(out=c_raw[:, i, :], in_=rows[ch, i])
+            return c_raw
+
+        x_tiles = [load_unit(*units[0])]
+
+        w_words = keep.tile([P, 2, IN_PASSES, FEAT], U32, align_bytes=64)
+        w_scales = keep.tile([P, 2, IN_PASSES, FEAT], U8, align_bytes=64)
+        nc.vector.memset(w_scales[:].bitcast(I32), 0)
+        bias_rows = keep.tile([P, P], BF16)
+        nc.vector.memset(bias_rows[:], 0.0)
+        for w, (words, scales, bias) in enumerate(
+            ((W_f_words, W_f_scales, b_f), (W_r_words, W_r_scales, b_r))
+        ):
+            for g in range(IN_PASSES):
+                nc.sync.dma_start(
+                    out=w_words[:, w, g, :].bitcast(I32),
+                    in_=words[g].rearrange("p n t -> p (n t)").bitcast(I32),
+                )
+            for quadrant in range(4):
+                nc.sync.dma_start(
+                    out=w_scales[32 * quadrant : 32 * quadrant + 4, w, :, :].bitcast(I32),
+                    in_=scales[:, 4 * quadrant : 4 * quadrant + 4, :]
+                    .rearrange("g r n -> r g n")
+                    .bitcast(I32),
+                )
+            nc.sync.dma_start(
+                out=bias_rows[PACK * w : PACK * (w + 1), :],
+                in_=bias.rearrange("(t p) -> t p", p=P),
+            )
+
+        c_tiles = [load_centre_half(0)]
+        x_tiles.append(load_unit(*units[1]))
+        c_tiles.append(load_centre_half(1))
+        for h, v in units[2:]:
+            x_tiles.append(load_unit(h, v))
+
+        ident_f32 = keep.tile([P, P], F32)
+        make_identity(nc, ident_f32[:])
+        ident_bf16 = keep.tile([P, P], BF16)
+        make_identity(nc, ident_bf16[:])
+
+        one = keep.tile([P, 1], F32)
+        nc.vector.memset(one[:], 1.0)
+        root_of_one = keep.tile([P, 1], F32)
+        nc.scalar.activation(out=root_of_one[:], in_=one[:], func=ACT.Sqrt)
+
+        bias_ps = psum.tile([P, P], BF16, tag="tp", bufs=3)
+        nc.tensor.transpose(bias_ps[:], bias_rows[:], ident_bf16[:])
+        bias_cols = keep.tile([P, 2 * PACK], F32)
+        nc.vector.tensor_copy(out=bias_cols[:], in_=bias_ps[:, 0 : 2 * PACK])
+
+        c_words = keep.tile([P, VIEWS, NCLASS], U32, align_bytes=64)
+        c_scales = keep.tile([P, VIEWS, NCLASS], U8, align_bytes=64)
+        c2_cols = keep.tile([P, NCLASS // P], F32)
+        c2_rows = keep.tile([P, NCLASS], F32)
+        f2_parts = keep.tile([P, HALVES * ROW_TILES, VIEWS], F32)
+        f2_cols = keep.tile([P, HALVES * ROW_TILES], F32)
+
+        def quantise_unit(raw):
+            x_words = stream.tile([P, IN_PASSES, BANK], U32, tag="x_words", align_bytes=64)
+            x_scales = stream.tile([P, IN_PASSES, BANK], U8, tag="x_scales", align_bytes=64)
+            for g in range(IN_PASSES):
+                x_grp = stream.tile([P, BANK, PACK], BF16, tag="x_grp", bufs=3, align_bytes=64)
+                for pair in range(ROW_TILES // 2):
+                    xt = psum.tile([P, 2, 2 * P], F32, tag="tp", bufs=3)
+                    for jj in range(2):
+                        x_pairs = raw[:, 2 * pair + jj, :].bitcast(F32)
+                        for u in range(2):
+                            nc.tensor.transpose(
+                                xt[:, u, jj * P : (jj + 1) * P],
+                                x_pairs[:, 256 * g + u : 256 * (g + 1) : 2],
+                                ident_f32[:],
+                            )
+                    nc.vector.tensor_copy(
+                        out=x_grp[:, 2 * P * pair : 2 * P * (pair + 1), :].bitcast(F32),
+                        in_=xt[:].rearrange("p u b -> p b u"),
+                    )
+                nc.vector.quantize_mx(
+                    out=x_words[:, g, :].bitcast(FP8X4),
+                    scales=x_scales[:, g, :],
+                    in_=x_grp[:].rearrange("p b t -> p (b t)"),
+                )
+            return x_words, x_scales
+
+        def quantise_centre_block(ch, g):
+            c_grp = stream.tile([P, BANK, PACK], BF16, tag="c_grp", align_bytes=64)
+            for pair in range(ROW_TILES // 2):
+                ct = psum.tile([P, PACK, 2 * P], BF16, tag="tp", bufs=3)
+                for ii in range(2):
+                    for t in range(PACK):
+                        first = K_PASS * g + P * t
+                        nc.tensor.transpose(
+                            ct[:, t, ii * P : (ii + 1) * P],
+                            c_tiles[ch][:, 2 * pair + ii, first : first + P],
+                            ident_bf16[:],
+                        )
+                copy = nc.scalar.copy if pair == 0 else nc.vector.tensor_copy
+                copy(
+                    out=c_grp[:, 2 * P * pair : 2 * P * (pair + 1), :],
+                    in_=ct[:].rearrange("p t c -> p c t"),
+                )
+            nc.vector.quantize_mx(
+                out=c_words[:, g, BANK * ch : BANK * (ch + 1)].bitcast(FP8X4),
+                scales=c_scales[:, g, BANK * ch : BANK * (ch + 1)],
+                in_=c_grp[:].rearrange("p c t -> p (c t)"),
+            )
+            c_sq = stream.tile([P, D], BF16, tag="c_sq")
+            i = ROW_TILES * ch + g
+            nc.scalar.activation(
+                out=c_sq[:], in_=c_tiles[ch][:, g, :], func=ACT.Square, accum_out=c2_cols[:, i : i + 1]
+            )
+
+        def spread_c2():
+            for ch in range(CENTRE_HALVES):
+                c2_ps = psum.tile([P, BANK], F32, tag="tp", bufs=3)
+                for ii in range(ROW_TILES):
+                    i = ROW_TILES * ch + ii
+                    nc.tensor.transpose(
+                        c2_ps[:, ii * P : (ii + 1) * P],
+                        c2_cols[:, i : i + 1].to_broadcast([P, P]),
+                        ident_f32[:],
+                    )
+                nc.vector.tensor_copy(out=c2_rows[:, BANK * ch : BANK * (ch + 1)], in_=c2_ps[:])
+
+        def project_unit(v, x_words, x_scales, f_words, f_scales):
+            w = weight_of_view[v]
+            feat = stream.tile([P, PACK, BANK], F32, tag="feat", bufs=3)
+            for t in range(PACK):
+                acc = psum.tile([P, BANK], F32, tag="s1", bufs=3)
+                for g in range(IN_PASSES):
+                    nc.tensor.matmul_mx(
+                        out=acc[:],
+                        lhsT=w_words[:, w, g, t * P : (t + 1) * P].bitcast(FP8X4),
+                        lhsT_scale=w_scales[:, w, g, t * P : (t + 1) * P],
+                        rhs=x_words[:, g, :].bitcast(FP8X4),
+                        rhs_scale=x_scales[:, g, :],
+                        start=(g == 0),
+                        stop=(g == IN_PASSES - 1),
+                    )
+                col = PACK * w + t
+                nc.scalar.activation(
+                    out=feat[:, t, :], in_=acc[:], func=ACT.Relu, bias=bias_cols[:, col : col + 1]
+                )
+            f_grp = stream.tile([P, BANK, PACK], BF16, tag="f_grp", align_bytes=64)
+            nc.vector.tensor_copy(out=f_grp[:], in_=feat[:].rearrange("p t b -> p b t"))
+            nc.vector.quantize_mx(
+                out=f_words[:, v, :].bitcast(FP8X4),
+                scales=f_scales[:, v, :],
+                in_=f_grp[:].rearrange("p b t -> p (b t)"),
+            )
+            return feat
+
+        def sum_squares(h, v, feat):
+            for j in range(ROW_TILES):
+                ft = psum.tile([P, BANK], F32, tag="tp", bufs=3)
+                for t in range(PACK):
+                    nc.tensor.transpose(
+                        ft[:, t * P : (t + 1) * P], feat[:, t, j * P : (j + 1) * P], ident_f32[:]
+                    )
+                f_sq = stream.tile([P, BANK], BF16, tag="f_sq")
+                nc.scalar.activation(
+                    out=f_sq[:],
+                    in_=ft[:],
+                    func=ACT.Square,
+                    accum_out=f2_parts[:, ROW_TILES * h + j, v : v + 1],
+                )
+
+        def score_rows(h, j, f_words, f_scales):
+            row = ROW_TILES * h + j
+            nc.vector.tensor_reduce(
+                out=f2_cols[:, row : row + 1],
+                in_=f2_parts[:, row, :],
+                axis=mybir.AxisListType.X,
+                op=ALU.add,
+            )
+            scores = stream.tile([P, NCLASS], F32, tag="scores", bufs=3)
+            for ch in range(CENTRE_HALVES):
+                cols = slice(BANK * ch, BANK * (ch + 1))
+                cross = psum.tile([P, BANK], F32, tag="s2", bufs=2)
+                for v in range(VIEWS):
+                    nc.tensor.matmul_mx(
+                        out=cross[:],
+                        lhsT=f_words[:, v, j * P : (j + 1) * P].bitcast(FP8X4),
+                        lhsT_scale=f_scales[:, v, j * P : (j + 1) * P],
+                        rhs=c_words[:, v, cols].bitcast(FP8X4),
+                        rhs_scale=c_scales[:, v, cols],
+                        start=(v == 0),
+                        stop=(v == VIEWS - 1),
+                    )
+                d2 = stream.tile([P, BANK], F32, tag="d2", bufs=3)
+                nc.vector.scalar_tensor_tensor(
+                    out=d2[:], in0=cross[:], scalar=-2.0, in1=c2_rows[:, cols], op0=ALU.mult, op1=ALU.add
+                )
+                nc.vector.tensor_scalar(
+                    out=d2[:],
+                    in0=d2[:],
+                    scalar1=f2_cols[:, row : row + 1],
+                    scalar2=0.0,
+                    op0=ALU.add,
+                    op1=ALU.max,
+                )
+                dist = stream.tile([P, BANK], F32, tag="dist", bufs=3)
+                nc.scalar.activation(out=dist[:], in_=d2[:], func=ACT.Sqrt)
+                nc.vector.tensor_scalar_mul(out=scores[:, cols], in0=dist[:], scalar1=-GAMMA)
+            out_rows = out.rearrange("(h p j) c -> h j p c", h=HALVES, p=P)
+            nc.sync.dma_start(out=out_rows[h, j], in_=scores[:])
+
+        quantised = {}
+        feats = {}
+        f_operands = {}
+        last_step = UNITS - 1 + NORM_LAG + ROW_TILES - 1
+        for step in range(last_step + 1):
+            if step < UNITS:
+                quantised[step] = quantise_unit(x_tiles[step])
+            for block in range(BLOCKS_PER_STEP * step, BLOCKS_PER_STEP * (step + 1)):
+                if block < CENTRE_BLOCKS:
+                    quantise_centre_block(block // VIEWS, block % VIEWS)
+            if step == CENTRE_BLOCKS // BLOCKS_PER_STEP:
+                spread_c2()
+            if 0 <= step - NORM_LAG < UNITS:
+                h, v = units[step - NORM_LAG]
+                sum_squares(h, v, feats[step - NORM_LAG])
+            if 0 <= step - PROJECT_LAG < UNITS:
+                h, v = units[step - PROJECT_LAG]
+                if v == 0:
+                    f_words = stream.tile([P, VIEWS, BANK], U32, tag="f_words", align_bytes=64)
+                    f_scales = stream.tile([P, VIEWS, BANK], U8, tag="f_scales", align_bytes=64)
+                    f_operands[h] = (f_words, f_scales)
+                feats[step - PROJECT_LAG] = project_unit(v, *quantised[step - PROJECT_LAG], *f_operands[h])
+            for h in range(HALVES):
+                j = step - (VIEWS * (h + 1) - 1 + NORM_LAG)
+                if 0 <= j < ROW_TILES:
+                    score_rows(h, j, *f_operands[h])

@@ -22,15 +22,22 @@ VIEWS = 4
 D = VIEWS * FEAT
 GAMMA = 0.1
 
-HALVES = BATCH // BANK
-ROW_TILES = BANK // P
+ROWS = 256
+CHUNKS = BATCH // ROWS
+ROW_TILES = ROWS // P
 IN_PASSES = IN_F // K_PASS
-UNITS = HALVES * VIEWS
+UNITS = CHUNKS * VIEWS
+PARTS = 2
+CENTRE_TILES = BANK // P
 CENTRE_HALVES = NCLASS // BANK
-CENTRE_BLOCKS = CENTRE_HALVES * VIEWS
-BLOCKS_PER_STEP = 2
-PROJECT_LAG = 1
-NORM_LAG = 2
+CENTRE_PAIRS = NCLASS // (2 * P)
+
+QUANT_LAG = 1
+PROJECT_LAG = 2
+RELU_LAG = 3
+LAYOUT_LAG = 4
+FEAT_QUANT_LAG = 5
+NORM_LAG = 5
 
 FLOPS = 2 * BATCH * IN_F * FEAT * VIEWS + 2 * BATCH * D * NCLASS
 
@@ -41,205 +48,270 @@ def tile_qccpn_pa_kernel(
     nc = tc.nc
     views = [x, x_90, x_180, x_270]
     weight_of_view = [0, 1, 1, 1]
-    units = [(h, v) for h in range(HALVES) for v in range(VIEWS)]
+    units = [(h, v) for h in range(CHUNKS) for v in range(VIEWS)]
 
     with ExitStack() as stack:
         keep = stack.enter_context(tc.tile_pool(name="keep", bufs=1))
         stream = stack.enter_context(tc.tile_pool(name="stream", bufs=2))
         psum = stack.enter_context(tc.psum_pool(name="psum", bufs=2))
-
-        def load_unit(h, v):
-            x_raw = stream.tile([P, ROW_TILES, IN_F], BF16, tag="x_raw", bufs=4)
-            rows = views[v].rearrange("(h p j) k -> h p j k", h=HALVES, p=P)
-            nc.sync.dma_start(out=x_raw[:], in_=rows[h])
-            return x_raw
-
-        def load_centre_half(ch):
-            c_raw = stream.tile([P, ROW_TILES, D], BF16, tag="c_raw", bufs=CENTRE_HALVES)
-            rows = centers.rearrange("(ch i p) k -> ch i p k", ch=CENTRE_HALVES, p=P)
-            for i in range(ROW_TILES):
-                nc.sync.dma_start(out=c_raw[:, i, :], in_=rows[ch, i])
-            return c_raw
-
-        x_tiles = [load_unit(*units[0])]
-
-        w_words = keep.tile([P, 2, IN_PASSES, FEAT], U32, align_bytes=64)
-        w_scales = keep.tile([P, 2, IN_PASSES, FEAT], U8, align_bytes=64)
-        nc.vector.memset(w_scales[:].bitcast(I32), 0)
-        bias_rows = keep.tile([P, P], BF16)
-        nc.vector.memset(bias_rows[:], 0.0)
-        for w, (words, scales, bias) in enumerate(
-            ((W_f_words, W_f_scales, b_f), (W_r_words, W_r_scales, b_r))
-        ):
-            for g in range(IN_PASSES):
-                nc.sync.dma_start(
-                    out=w_words[:, w, g, :].bitcast(I32),
-                    in_=words[g].rearrange("p n t -> p (n t)").bitcast(I32),
-                )
-            for quadrant in range(4):
-                nc.sync.dma_start(
-                    out=w_scales[32 * quadrant : 32 * quadrant + 4, w, :, :].bitcast(I32),
-                    in_=scales[:, 4 * quadrant : 4 * quadrant + 4, :]
-                    .rearrange("g r n -> r g n")
-                    .bitcast(I32),
-                )
-            nc.sync.dma_start(
-                out=bias_rows[PACK * w : PACK * (w + 1), :],
-                in_=bias.rearrange("(t p) -> t p", p=P),
-            )
-
-        c_tiles = [load_centre_half(0)]
-        x_tiles.append(load_unit(*units[1]))
-        c_tiles.append(load_centre_half(1))
-        for h, v in units[2:]:
-            x_tiles.append(load_unit(h, v))
+        stack.enter_context(tc.manual_schedule())
 
         ident_f32 = keep.tile([P, P], F32)
         make_identity(nc, ident_f32[:])
-        ident_bf16 = keep.tile([P, P], BF16)
-        make_identity(nc, ident_bf16[:])
 
         one = keep.tile([P, 1], F32)
         nc.vector.memset(one[:], 1.0)
         root_of_one = keep.tile([P, 1], F32)
         nc.scalar.activation(out=root_of_one[:], in_=one[:], func=ACT.Sqrt)
 
-        bias_ps = psum.tile([P, P], BF16, tag="tp", bufs=3)
-        nc.tensor.transpose(bias_ps[:], bias_rows[:], ident_bf16[:])
-        bias_cols = keep.tile([P, 2 * PACK], F32)
-        nc.vector.tensor_copy(out=bias_cols[:], in_=bias_ps[:, 0 : 2 * PACK])
+        def load_unit(h, v, pieces):
+            x_raw = stream.tile([P, ROW_TILES, IN_F], BF16, tag="x_raw", bufs=10)
+            rows = views[v].rearrange("(h p j) k -> h p j k", h=CHUNKS, p=P)
+            n = ROW_TILES // pieces
+            for i in range(pieces):
+                nc.sync.dma_start(out=x_raw[:, i * n : (i + 1) * n, :], in_=rows[h][:, i * n : (i + 1) * n, :])
+            return x_raw
+
+        def load_centre_pair(cp):
+            c_raw = stream.tile([P, 2, D], BF16, tag="c_raw", bufs=CENTRE_PAIRS)
+            rows = centers.rearrange("(cp i p) k -> cp i p k", cp=CENTRE_PAIRS, p=P)
+            for i in range(2):
+                nc.sync.dma_start(out=c_raw[:, i, :], in_=rows[cp, i])
+            return c_raw
+
+        w_raw = [keep.tile([P, IN_PASSES, FEAT], U32, align_bytes=64, name="w_raw%d" % w) for w in range(2)]
+        s_raw = [keep.tile([P, FEAT], U8, align_bytes=64, name="s_raw%d" % w) for w in range(2)]
+        bias_rows = keep.tile([P, 2 * P], BF16)
+        for w in range(2):
+            nc.vector.memset(s_raw[w][:].bitcast(I32), 0)
+        nc.vector.memset(bias_rows[:], 0.0)
+
+        def load_weight(w):
+            words, scales = ((W_f_words, W_f_scales), (W_r_words, W_r_scales))[w]
+            nc.sync.dma_start(
+                out=w_raw[w][:].bitcast(I32),
+                in_=words.rearrange("g p n t -> p g (n t)").bitcast(I32),
+            )
+            for quadrant in range(4):
+                nc.sync.dma_start(
+                    out=s_raw[w][32 * quadrant : 32 * quadrant + 4 * IN_PASSES, :].bitcast(I32),
+                    in_=scales[:, 4 * quadrant : 4 * quadrant + 4, :].bitcast(I32),
+                )
+
+        def load_biases():
+            for w, bias in enumerate((b_f, b_r)):
+                nc.sync.dma_start(out=bias_rows[2 * w : 2 * w + 2, :], in_=bias.rearrange("(u m) -> u m", u=2))
+
+        x_tiles = [load_unit(*units[0], 2), load_unit(*units[1], 1)]
+        load_weight(0)
+        load_biases()
+        load_weight(1)
+        c_tiles = [load_centre_pair(0)]
+        x_tiles.append(load_unit(*units[2], 1))
+        x_tiles.append(load_unit(*units[3], 1))
+        c_tiles.append(load_centre_pair(1))
+        for h, v in units[4:6]:
+            x_tiles.append(load_unit(h, v, 1))
+        c_tiles.append(load_centre_pair(2))
+        for h, v in units[6:8]:
+            x_tiles.append(load_unit(h, v, 1))
+        c_tiles.append(load_centre_pair(3))
+        for h, v in units[8:]:
+            x_tiles.append(load_unit(h, v, 1))
+
+        w_words = keep.tile([P, 2, IN_PASSES, FEAT], U32, align_bytes=64)
+        w_scales = keep.tile([P, 2, FEAT], U8, align_bytes=64)
+        bias_cols = keep.tile([P, 2, 2, 2], F32)
+
+        def permute_weight(w, u):
+            cols = slice(2 * P * u, 2 * P * (u + 1))
+            nc.vector.tensor_copy(
+                out=w_words[:, w, :, cols].bitcast(I32).rearrange("p g (e m) -> p g e m", e=2),
+                in_=w_raw[w][:, :, cols].bitcast(I32).rearrange("p g (m e) -> p g e m", e=2),
+            )
+            nc.vector.tensor_copy(
+                out=w_scales[:, w, cols].rearrange("p (e m) -> p e m", e=2),
+                in_=s_raw[w][:, cols].rearrange("p (m e) -> p e m", e=2),
+            )
+
+        def spread_bias():
+            bias_ps = psum.tile([P, P], F32, tag="tc", bufs=2)
+            nc.tensor.transpose(bias_ps[:], bias_rows[:].bitcast(F32), ident_f32[:])
+            nc.vector.tensor_copy(
+                out=bias_cols[:].rearrange("p w u e -> p (w u e)"), in_=bias_ps[:].bitcast(BF16)[:, 0:8]
+            )
 
         c_words = keep.tile([P, VIEWS, NCLASS], U32, align_bytes=64)
         c_scales = keep.tile([P, VIEWS, NCLASS], U8, align_bytes=64)
+        c2_parts = keep.tile([P, NCLASS // P, 2], F32)
         c2_cols = keep.tile([P, NCLASS // P], F32)
         c2_rows = keep.tile([P, NCLASS], F32)
-        f2_parts = keep.tile([P, HALVES * ROW_TILES, VIEWS], F32)
-        f2_cols = keep.tile([P, HALVES * ROW_TILES], F32)
+        f2_parts = keep.tile([P, CHUNKS * ROW_TILES, VIEWS], F32)
+        f2_cols = keep.tile([P, CHUNKS * ROW_TILES], F32)
 
-        def quantise_unit(raw):
-            x_words = stream.tile([P, IN_PASSES, BANK], U32, tag="x_words", align_bytes=64)
-            x_scales = stream.tile([P, IN_PASSES, BANK], U8, tag="x_scales", align_bytes=64)
-            for g in range(IN_PASSES):
-                x_grp = stream.tile([P, BANK, PACK], BF16, tag="x_grp", bufs=3, align_bytes=64)
-                for pair in range(ROW_TILES // 2):
-                    xt = psum.tile([P, 2, 2 * P], F32, tag="tp", bufs=3)
-                    for jj in range(2):
-                        x_pairs = raw[:, 2 * pair + jj, :].bitcast(F32)
-                        for u in range(2):
-                            nc.tensor.transpose(
-                                xt[:, u, jj * P : (jj + 1) * P],
-                                x_pairs[:, 256 * g + u : 256 * (g + 1) : 2],
-                                ident_f32[:],
-                            )
-                    nc.vector.tensor_copy(
-                        out=x_grp[:, 2 * P * pair : 2 * P * (pair + 1), :].bitcast(F32),
-                        in_=xt[:].rearrange("p u b -> p b u"),
-                    )
-                nc.vector.quantize_mx(
-                    out=x_words[:, g, :].bitcast(FP8X4),
-                    scales=x_scales[:, g, :],
-                    in_=x_grp[:].rearrange("p b t -> p (b t)"),
-                )
-            return x_words, x_scales
+        x_banks, x_groups, x_operands = {}, {}, {}
+        c_banks, c_groups = {}, {}
+        s1_banks, feats, f_groups, f_banks, f_operands = {}, {}, {}, {}, {}
+        score_banks, d2_tiles, dist_tiles = {}, {}, {}
 
-        def quantise_centre_block(ch, g):
-            c_grp = stream.tile([P, BANK, PACK], BF16, tag="c_grp", align_bytes=64)
-            for pair in range(ROW_TILES // 2):
-                ct = psum.tile([P, PACK, 2 * P], BF16, tag="tp", bufs=3)
-                for ii in range(2):
-                    for t in range(PACK):
-                        first = K_PASS * g + P * t
-                        nc.tensor.transpose(
-                            ct[:, t, ii * P : (ii + 1) * P],
-                            c_tiles[ch][:, 2 * pair + ii, first : first + P],
-                            ident_bf16[:],
-                        )
-                copy = nc.scalar.copy if pair == 0 else nc.vector.tensor_copy
-                copy(
-                    out=c_grp[:, 2 * P * pair : 2 * P * (pair + 1), :],
-                    in_=ct[:].rearrange("p t c -> p c t"),
-                )
-            nc.vector.quantize_mx(
-                out=c_words[:, g, BANK * ch : BANK * (ch + 1)].bitcast(FP8X4),
-                scales=c_scales[:, g, BANK * ch : BANK * (ch + 1)],
-                in_=c_grp[:].rearrange("p c t -> p (c t)"),
-            )
-            c_sq = stream.tile([P, D], BF16, tag="c_sq")
-            i = ROW_TILES * ch + g
-            nc.scalar.activation(
-                out=c_sq[:], in_=c_tiles[ch][:, g, :], func=ACT.Square, accum_out=c2_cols[:, i : i + 1]
-            )
-
-        def spread_c2():
-            for ch in range(CENTRE_HALVES):
-                c2_ps = psum.tile([P, BANK], F32, tag="tp", bufs=3)
-                for ii in range(ROW_TILES):
-                    i = ROW_TILES * ch + ii
+        def transpose_x(u, g):
+            xt = psum.tile([P, 2, ROWS], F32, tag="tx", bufs=2)
+            for j in range(ROW_TILES):
+                words = x_tiles[u][:, j, :].bitcast(F32)
+                for e in range(2):
                     nc.tensor.transpose(
-                        c2_ps[:, ii * P : (ii + 1) * P],
-                        c2_cols[:, i : i + 1].to_broadcast([P, P]),
+                        xt[:, e, j * P : (j + 1) * P],
+                        words[:, 256 * g + e : 256 * (g + 1) : 2],
                         ident_f32[:],
                     )
-                nc.vector.tensor_copy(out=c2_rows[:, BANK * ch : BANK * (ch + 1)], in_=c2_ps[:])
+            x_banks[u, g] = xt
 
-        def project_unit(v, x_words, x_scales, f_words, f_scales):
-            w = weight_of_view[v]
-            feat = stream.tile([P, PACK, BANK], F32, tag="feat", bufs=3)
-            for t in range(PACK):
-                acc = psum.tile([P, BANK], F32, tag="s1", bufs=3)
+        def copy_x(u, g):
+            x_grp = stream.tile([P, ROWS, PACK], BF16, tag="x_grp", bufs=3, align_bytes=64)
+            x_groups[u, g] = x_grp
+            nc.vector.tensor_copy(out=x_grp[:].bitcast(F32), in_=x_banks.pop((u, g))[:].rearrange("p e b -> p b e"))
+
+        def quantise_x(u, g):
+            if g == 0:
+                x_words = stream.tile([P, IN_PASSES, ROWS], U32, tag="x_words", bufs=3, align_bytes=64)
+                x_scales = stream.tile([P, IN_PASSES, ROWS], U8, tag="x_scales", bufs=3, align_bytes=64)
+                x_operands[u] = (x_words, x_scales)
+            x_words, x_scales = x_operands[u]
+            nc.vector.quantize_mx(
+                out=x_words[:, g, :].bitcast(FP8X4),
+                scales=x_scales[:, g, :],
+                in_=x_groups.pop((u, g))[:].rearrange("p b t -> p (b t)"),
+            )
+
+        def transpose_c(cp, v):
+            ct = psum.tile([P, 2, 2 * P], F32, tag="tc", bufs=2)
+            for i in range(2):
+                words = c_tiles[cp][:, i, :].bitcast(F32)
+                for u in range(2):
+                    first = 256 * v + P * u
+                    nc.tensor.transpose(
+                        ct[:, u, i * P : (i + 1) * P], words[:, first : first + P], ident_f32[:]
+                    )
+            c_banks[cp, v] = ct
+
+        def copy_c(cp, v):
+            c_grp = stream.tile([P, 2 * P, PACK], BF16, tag="c_grp", align_bytes=64)
+            c_groups[cp, v] = c_grp
+            copy = nc.scalar.copy if cp >= 2 and v % 2 == 1 else nc.vector.tensor_copy
+            copy(
+                out=c_grp[:].bitcast(F32),
+                in_=c_banks.pop((cp, v))[:].rearrange("p u c -> p c u"),
+            )
+
+        def quantise_c(cp, v):
+            cols = slice(2 * P * cp, 2 * P * (cp + 1))
+            nc.vector.quantize_mx(
+                out=c_words[:, v, cols].bitcast(FP8X4),
+                scales=c_scales[:, v, cols],
+                in_=c_groups.pop((cp, v))[:].rearrange("p c t -> p (c t)"),
+            )
+
+        def square_c(i, half):
+            c_sq = stream.tile([P, D // 2], BF16, tag="c_sq")
+            nc.scalar.activation(
+                out=c_sq[:],
+                in_=c_tiles[i // 2][:, i % 2, half * (D // 2) : (half + 1) * (D // 2)],
+                func=ACT.Square,
+                accum_out=c2_parts[:, i, half : half + 1],
+            )
+
+        def sum_c2(cp):
+            tiles = slice(2 * cp, 2 * cp + 2)
+            nc.vector.tensor_reduce(
+                out=c2_cols[:, tiles], in_=c2_parts[:, tiles, :], axis=mybir.AxisListType.X, op=ALU.add
+            )
+
+        def transpose_c2(cp):
+            c2_ps = psum.tile([P, 2 * P], F32, tag="tc", bufs=2)
+            for i in range(2):
+                column = c2_cols[:, 2 * cp + i : 2 * cp + i + 1]
+                nc.tensor.transpose(c2_ps[:, i * P : (i + 1) * P], column.to_broadcast([P, P]), ident_f32[:])
+            c_banks[cp] = c2_ps
+
+        def copy_c2(cp):
+            nc.vector.tensor_copy(out=c2_rows[:, 2 * P * cp : 2 * P * (cp + 1)], in_=c_banks.pop(cp)[:])
+
+        def project(u, k):
+            w = weight_of_view[units[u][1]]
+            acc = psum.tile([P, 2, ROWS], F32, tag="s1", bufs=2)
+            for i in range(2):
+                cols = slice((2 * k + i) * P, (2 * k + i + 1) * P)
                 for g in range(IN_PASSES):
                     nc.tensor.matmul_mx(
-                        out=acc[:],
-                        lhsT=w_words[:, w, g, t * P : (t + 1) * P].bitcast(FP8X4),
-                        lhsT_scale=w_scales[:, w, g, t * P : (t + 1) * P],
-                        rhs=x_words[:, g, :].bitcast(FP8X4),
-                        rhs_scale=x_scales[:, g, :],
+                        out=acc[:, i, :],
+                        lhsT=w_words[:, w, g, cols].bitcast(FP8X4),
+                        lhsT_scale=w_scales[4 * g : P, w, cols],
+                        rhs=x_operands[u][0][:, g, :].bitcast(FP8X4),
+                        rhs_scale=x_operands[u][1][:, g, :],
                         start=(g == 0),
                         stop=(g == IN_PASSES - 1),
                     )
-                col = PACK * w + t
+            s1_banks[u, k] = acc
+
+        def relu(u, k):
+            w = weight_of_view[units[u][1]]
+            if k == 0:
+                feat = stream.tile([P, PACK, ROWS], F32, tag="feat", bufs=4)
+                feats[u] = feat
+            acc = s1_banks.pop((u, k))
+            for i in range(2):
                 nc.scalar.activation(
-                    out=feat[:, t, :], in_=acc[:], func=ACT.Relu, bias=bias_cols[:, col : col + 1]
+                    out=feats[u][:, 2 * k + i, :], in_=acc[:, i, :], func=ACT.Relu, bias=bias_cols[:, w, k, i : i + 1]
                 )
-            f_grp = stream.tile([P, BANK, PACK], BF16, tag="f_grp", align_bytes=64)
-            nc.vector.tensor_copy(out=f_grp[:], in_=feat[:].rearrange("p t b -> p b t"))
+
+        def lay_out_feat(u):
+            f_grp = stream.tile([P, ROWS, PACK], BF16, tag="f_grp", align_bytes=64)
+            f_groups[u] = f_grp
+            nc.vector.tensor_copy(out=f_grp[:], in_=feats[u][:].rearrange("p t b -> p b t"))
+
+        def quantise_feat(u):
+            h, v = units[u]
+            if v == 0:
+                f_words = stream.tile([P, VIEWS, ROWS], U32, tag="f_words", bufs=3, align_bytes=64)
+                f_scales = stream.tile([P, VIEWS, ROWS], U8, tag="f_scales", bufs=3, align_bytes=64)
+                f_operands[h] = (f_words, f_scales)
+            f_words, f_scales = f_operands[h]
             nc.vector.quantize_mx(
                 out=f_words[:, v, :].bitcast(FP8X4),
                 scales=f_scales[:, v, :],
-                in_=f_grp[:].rearrange("p b t -> p (b t)"),
+                in_=f_groups.pop(u)[:].rearrange("p b t -> p (b t)"),
             )
-            return feat
 
-        def sum_squares(h, v, feat):
-            for j in range(ROW_TILES):
-                ft = psum.tile([P, BANK], F32, tag="tp", bufs=3)
-                for t in range(PACK):
-                    nc.tensor.transpose(
-                        ft[:, t * P : (t + 1) * P], feat[:, t, j * P : (j + 1) * P], ident_f32[:]
-                    )
-                f_sq = stream.tile([P, BANK], BF16, tag="f_sq")
-                nc.scalar.activation(
-                    out=f_sq[:],
-                    in_=ft[:],
-                    func=ACT.Square,
-                    accum_out=f2_parts[:, ROW_TILES * h + j, v : v + 1],
-                )
+        def transpose_feat(u, j):
+            ft = psum.tile([P, BANK], F32, tag="tf", bufs=2)
+            for t in range(PACK):
+                nc.tensor.transpose(ft[:, t * P : (t + 1) * P], feats[u][:, t, j * P : (j + 1) * P], ident_f32[:])
+            f_banks[u, j] = ft
 
-        def score_rows(h, j, f_words, f_scales):
-            row = ROW_TILES * h + j
+        def square_feat(u, j):
+            h, v = units[u]
+            f_sq = stream.tile([P, BANK], BF16, tag="f_sq")
+            nc.scalar.activation(
+                out=f_sq[:],
+                in_=f_banks.pop((u, j))[:],
+                func=ACT.Square,
+                accum_out=f2_parts[:, ROW_TILES * h + j, v : v + 1],
+            )
+
+        def sum_f2(h):
+            rows = slice(ROW_TILES * h, ROW_TILES * (h + 1))
             nc.vector.tensor_reduce(
-                out=f2_cols[:, row : row + 1],
-                in_=f2_parts[:, row, :],
-                axis=mybir.AxisListType.X,
-                op=ALU.add,
+                out=f2_cols[:, rows], in_=f2_parts[:, rows, :], axis=mybir.AxisListType.X, op=ALU.add
             )
-            scores = stream.tile([P, NCLASS], F32, tag="scores", bufs=3)
-            for ch in range(CENTRE_HALVES):
-                cols = slice(BANK * ch, BANK * (ch + 1))
-                cross = psum.tile([P, BANK], F32, tag="s2", bufs=2)
+
+        def score(h, cp):
+            cols = slice(2 * P * cp, 2 * P * (cp + 1))
+            f_words, f_scales = f_operands[h]
+            cross = psum.tile([P, ROW_TILES, 2 * P], F32, tag="tc", bufs=2)
+            for j in range(ROW_TILES):
                 for v in range(VIEWS):
                     nc.tensor.matmul_mx(
-                        out=cross[:],
+                        out=cross[:, j, :],
                         lhsT=f_words[:, v, j * P : (j + 1) * P].bitcast(FP8X4),
                         lhsT_scale=f_scales[:, v, j * P : (j + 1) * P],
                         rhs=c_words[:, v, cols].bitcast(FP8X4),
@@ -247,47 +319,124 @@ def tile_qccpn_pa_kernel(
                         start=(v == 0),
                         stop=(v == VIEWS - 1),
                     )
-                d2 = stream.tile([P, BANK], F32, tag="d2", bufs=3)
-                nc.vector.scalar_tensor_tensor(
-                    out=d2[:], in0=cross[:], scalar=-2.0, in1=c2_rows[:, cols], op0=ALU.mult, op1=ALU.add
-                )
+            score_banks[h, cp] = cross
+
+        def add_c2(h, cp):
+            d2 = stream.tile([P, ROW_TILES, 2 * P], F32, tag="d2", bufs=4)
+            nc.vector.scalar_tensor_tensor(
+                out=d2[:],
+                in0=score_banks.pop((h, cp))[:],
+                scalar=-2.0,
+                in1=c2_rows[:, 2 * P * cp : 2 * P * (cp + 1)].unsqueeze(1).to_broadcast([P, ROW_TILES, 2 * P]),
+                op0=ALU.mult,
+                op1=ALU.add,
+            )
+            d2_tiles[h, cp] = d2
+
+        def add_f2(h, cp):
+            d2 = d2_tiles[h, cp]
+            for j in range(ROW_TILES):
+                row = ROW_TILES * h + j
                 nc.vector.tensor_scalar(
-                    out=d2[:],
-                    in0=d2[:],
+                    out=d2[:, j, :],
+                    in0=d2[:, j, :],
                     scalar1=f2_cols[:, row : row + 1],
                     scalar2=0.0,
                     op0=ALU.add,
                     op1=ALU.max,
                 )
-                dist = stream.tile([P, BANK], F32, tag="dist", bufs=3)
-                nc.scalar.activation(out=dist[:], in_=d2[:], func=ACT.Sqrt)
-                nc.vector.tensor_scalar_mul(out=scores[:, cols], in0=dist[:], scalar1=-GAMMA)
-            out_rows = out.rearrange("(h p j) c -> h j p c", h=HALVES, p=P)
-            nc.sync.dma_start(out=out_rows[h, j], in_=scores[:])
 
-        quantised = {}
-        feats = {}
-        f_operands = {}
-        last_step = UNITS - 1 + NORM_LAG + ROW_TILES - 1
-        for step in range(last_step + 1):
-            if step < UNITS:
-                quantised[step] = quantise_unit(x_tiles[step])
-            for block in range(BLOCKS_PER_STEP * step, BLOCKS_PER_STEP * (step + 1)):
-                if block < CENTRE_BLOCKS:
-                    quantise_centre_block(block // VIEWS, block % VIEWS)
-            if step == CENTRE_BLOCKS // BLOCKS_PER_STEP:
-                spread_c2()
-            if 0 <= step - NORM_LAG < UNITS:
-                h, v = units[step - NORM_LAG]
-                sum_squares(h, v, feats[step - NORM_LAG])
-            if 0 <= step - PROJECT_LAG < UNITS:
-                h, v = units[step - PROJECT_LAG]
-                if v == 0:
-                    f_words = stream.tile([P, VIEWS, BANK], U32, tag="f_words", align_bytes=64)
-                    f_scales = stream.tile([P, VIEWS, BANK], U8, tag="f_scales", align_bytes=64)
-                    f_operands[h] = (f_words, f_scales)
-                feats[step - PROJECT_LAG] = project_unit(v, *quantised[step - PROJECT_LAG], *f_operands[h])
-            for h in range(HALVES):
-                j = step - (VIEWS * (h + 1) - 1 + NORM_LAG)
-                if 0 <= j < ROW_TILES:
-                    score_rows(h, j, *f_operands[h])
+        def root(h, cp):
+            dist = stream.tile([P, ROW_TILES, 2 * P], F32, tag="dist", bufs=4)
+            nc.scalar.activation(out=dist[:], in_=d2_tiles.pop((h, cp))[:], func=ACT.Sqrt)
+            dist_tiles[h, cp] = dist
+
+        def store(h, cp):
+            scores = stream.tile([P, ROW_TILES, 2 * P], F32, tag="scores", bufs=4)
+            nc.gpsimd.tensor_scalar(
+                out=scores[:],
+                in0=dist_tiles.pop((h, cp))[:],
+                scalar1=-GAMMA,
+                scalar2=0.0,
+                op0=ALU.mult,
+                op1=ALU.add,
+            )
+            out_rows = out.rearrange("(h p j) c -> h p j c", h=CHUNKS, p=P)
+            nc.sync.dma_start(out=out_rows[h][:, :, 2 * P * cp : 2 * P * (cp + 1)], in_=scores[:])
+
+        def part_of(step, lag):
+            k = step - lag
+            return divmod(k, PARTS) if 0 <= k < UNITS * PARTS else None
+
+        centre_at = [3, 4, 5, 6, 7, 8, 9, 10, 12, 14, 16, 18, 20, 22, 24, 26]
+        centre_jobs = {s: divmod(k, VIEWS) for k, s in enumerate(centre_at)}
+        square_at = [3, 4, 5, 6, 7, 8, 9, 10, 12, 14, 16, 18, 20, 22, 24, 26]
+        square_jobs = {s: divmod(k, 2) for k, s in enumerate(square_at)}
+        c2_steps = {7: 0, 11: 1, 19: 2, 27: 3}
+        score_order = [(0, 0), (0, 1), (0, 2), (1, 0), (1, 1), (1, 2), (0, 3), (1, 3), (2, 0), (2, 1), (2, 2), (2, 3), (3, 0), (3, 1), (3, 2), (3, 3)]
+        score_at = [13, 15, 20, 22, 24, 26, 28, 29, 30, 31, 33, 34, 36, 37, 38, 39]
+        score_steps = dict(zip(score_at, score_order))
+
+        for step in range(43):
+            norm = part_of(step, NORM_LAG)
+            if norm:
+                transpose_feat(*norm)
+            xs = part_of(step, 0)
+            if xs:
+                transpose_x(*xs)
+            if step in centre_jobs:
+                transpose_c(*centre_jobs[step])
+            if step - 1 in c2_steps:
+                transpose_c2(c2_steps[step - 1])
+
+            rel = part_of(step, RELU_LAG)
+            if rel:
+                relu(*rel)
+            if step - 1 in score_steps:
+                add_c2(*score_steps[step - 1])
+            fq = part_of(step, FEAT_QUANT_LAG)
+            if fq and fq[1] == 0:
+                quantise_feat(fq[0])
+            xq = part_of(step, QUANT_LAG)
+            if xq:
+                quantise_x(*xq)
+            if xs:
+                copy_x(*xs)
+            if norm:
+                square_feat(*norm)
+            if step in centre_jobs:
+                copy_c(*centre_jobs[step])
+            if step - 1 in c2_steps:
+                copy_c2(c2_steps[step - 1])
+            summed = part_of(step, NORM_LAG + 1)
+            if summed and units[summed[0]][1] == VIEWS - 1 and summed[1] == ROW_TILES - 1:
+                sum_f2(units[summed[0]][0])
+            if step - 1 in score_steps:
+                add_f2(*score_steps[step - 1])
+            if step - 1 in centre_jobs:
+                quantise_c(*centre_jobs[step - 1])
+            if step == 1:
+                permute_weight(0, 0)
+            if step == 2:
+                permute_weight(0, 1)
+                spread_bias()
+            if step == 3:
+                permute_weight(1, 0)
+                permute_weight(1, 1)
+            if step in square_jobs:
+                square_c(*square_jobs[step])
+            if step - 2 in score_steps:
+                root(*score_steps[step - 2])
+            lay = part_of(step, LAYOUT_LAG)
+            if lay and lay[1] == 0:
+                lay_out_feat(lay[0])
+            if step - 3 in score_steps:
+                store(*score_steps[step - 3])
+            if step in c2_steps:
+                sum_c2(c2_steps[step])
+
+            proj = part_of(step, PROJECT_LAG)
+            if proj:
+                project(*proj)
+            if step in score_steps:
+                score(*score_steps[step])

@@ -82,6 +82,8 @@ def tile_qccpn_pa_kernel(
         w_raw = [keep.tile([P, IN_PASSES, FEAT], U32, align_bytes=64, name="w_raw%d" % w) for w in range(2)]
         s_raw = [keep.tile([P, FEAT], U8, align_bytes=64, name="s_raw%d" % w) for w in range(2)]
         bias_rows = keep.tile([P, 2 * P], BF16)
+        warm = keep.tile([P, BANK], BF16)
+        nc.vector.memset(warm[:], 0.0)
         for w in range(2):
             nc.vector.memset(s_raw[w][:].bitcast(I32), 0)
         nc.vector.memset(bias_rows[:], 0.0)
@@ -236,9 +238,14 @@ def tile_qccpn_pa_kernel(
         def copy_c2(cp):
             nc.vector.tensor_copy(out=c2_rows[:, 2 * P * cp : 2 * P * (cp + 1)], in_=c_banks.pop(cp)[:])
 
-        def project(u, k):
+        def keep_warm(bank, n):
+            nc.tensor.matmul(out=bank, lhsT=warm[:, 0:P], rhs=warm[:, 0:n], start=True, stop=True)
+
+        def project(u, k, extra):
             w = weight_of_view[units[u][1]]
             acc = psum.tile([P, 2, ROWS], F32, tag="s1", bufs=2)
+            if extra:
+                keep_warm(acc[:].rearrange("p i b -> p (i b)"), BANK)
             for i in range(2):
                 cols = slice((2 * k + i) * P, (2 * k + i + 1) * P)
                 for g in range(IN_PASSES):
@@ -272,8 +279,8 @@ def tile_qccpn_pa_kernel(
         def quantise_feat(u):
             h, v = units[u]
             if v == 0:
-                f_words = stream.tile([P, VIEWS, ROWS], U32, tag="f_words", bufs=3, align_bytes=64)
-                f_scales = stream.tile([P, VIEWS, ROWS], U8, tag="f_scales", bufs=3, align_bytes=64)
+                f_words = stream.tile([P, VIEWS, ROWS], U32, tag="f_words", bufs=CHUNKS, align_bytes=64)
+                f_scales = stream.tile([P, VIEWS, ROWS], U8, tag="f_scales", bufs=CHUNKS, align_bytes=64)
                 f_operands[h] = (f_words, f_scales)
             f_words, f_scales = f_operands[h]
             nc.vector.quantize_mx(
@@ -368,16 +375,22 @@ def tile_qccpn_pa_kernel(
             k = step - lag
             return divmod(k, PARTS) if 0 <= k < UNITS * PARTS else None
 
-        centre_at = [3, 4, 5, 6, 7, 8, 9, 10, 12, 14, 16, 18, 20, 22, 24, 26]
+        centre_at = [3, 4, 5, 7, 8, 9, 11, 12, 13, 15, 16, 18, 20, 22, 24, 26]
         centre_jobs = {s: divmod(k, VIEWS) for k, s in enumerate(centre_at)}
-        square_at = [3, 4, 5, 6, 7, 8, 9, 10, 12, 14, 16, 18, 20, 22, 24, 26]
+        square_at = [3, 4, 5, 7, 8, 9, 11, 12, 13, 15, 16, 18, 20, 22, 24, 26]
         square_jobs = {s: divmod(k, 2) for k, s in enumerate(square_at)}
-        c2_steps = {7: 0, 11: 1, 19: 2, 27: 3}
+        c2_steps = {8: 0, 13: 1, 19: 2, 27: 3}
         score_order = [(0, 0), (0, 1), (0, 2), (1, 0), (1, 1), (1, 2), (0, 3), (1, 3), (2, 0), (2, 1), (2, 2), (2, 3), (3, 0), (3, 1), (3, 2), (3, 3)]
         score_at = [13, 15, 20, 22, 24, 26, 28, 29, 30, 31, 33, 34, 36, 37, 38, 39]
         score_steps = dict(zip(score_at, score_order))
 
-        for step in range(43):
+        warm_at = list(range(2, 13)) + list(range(16, 20))
+        warm_head = {0: 4, 1: 3, 2: 5, 3: 1, 4: 1, 5: 1, 6: 1}
+
+        for step in range(45):
+            for i in range(warm_head.get(step, 0)):
+                idle = psum.tile([P, BANK], F32, tag="tc", bufs=2)
+                keep_warm(idle[:], BANK)
             norm = part_of(step, NORM_LAG)
             if norm:
                 transpose_feat(*norm)
@@ -437,6 +450,6 @@ def tile_qccpn_pa_kernel(
 
             proj = part_of(step, PROJECT_LAG)
             if proj:
-                project(*proj)
+                project(*proj, step in warm_at)
             if step in score_steps:
                 score(*score_steps[step])

@@ -83,7 +83,6 @@ def tile_qccpn_pa_kernel(
         s_raw = [keep.tile([P, FEAT], U8, align_bytes=64, name="s_raw%d" % w) for w in range(2)]
         bias_rows = keep.tile([P, 2 * P], BF16)
         warm = keep.tile([P, BANK], BF16)
-        nc.vector.memset(warm[:], 0.0)
         for w in range(2):
             nc.vector.memset(s_raw[w][:].bitcast(I32), 0)
         nc.vector.memset(bias_rows[:], 0.0)
@@ -120,6 +119,8 @@ def tile_qccpn_pa_kernel(
         c_tiles.append(load_centre_pair(3))
         for h, v in units[8:]:
             x_tiles.append(load_unit(h, v, 1))
+
+        nc.vector.tensor_copy(out=warm[:], in_=x_tiles[0][:, 0, 0:BANK])
 
         w_words = keep.tile([P, 2, IN_PASSES, FEAT], U32, align_bytes=64)
         w_scales = keep.tile([P, 2, FEAT], U8, align_bytes=64)
@@ -360,14 +361,7 @@ def tile_qccpn_pa_kernel(
 
         def store(h, cp):
             scores = stream.tile([P, ROW_TILES, 2 * P], F32, tag="scores", bufs=4)
-            nc.gpsimd.tensor_scalar(
-                out=scores[:],
-                in0=dist_tiles.pop((h, cp))[:],
-                scalar1=-GAMMA,
-                scalar2=0.0,
-                op0=ALU.mult,
-                op1=ALU.add,
-            )
+            nc.vector.tensor_scalar_mul(out=scores[:], in0=dist_tiles.pop((h, cp))[:], scalar1=-GAMMA)
             out_rows = out.rearrange("(h p j) c -> h p j c", h=CHUNKS, p=P)
             nc.sync.dma_start(out=out_rows[h][:, :, 2 * P * cp : 2 * P * (cp + 1)], in_=scores[:])
 
@@ -385,7 +379,7 @@ def tile_qccpn_pa_kernel(
         score_steps = dict(zip(score_at, score_order))
 
         warm_at = list(range(2, 13)) + list(range(16, 20))
-        warm_head = {0: 4, 1: 3, 2: 5, 3: 1, 4: 1, 5: 1, 6: 1}
+        warm_head = {0: 0, 1: 3, 2: 5, 3: 1, 4: 1, 5: 1, 6: 1}
 
         for step in range(45):
             for i in range(warm_head.get(step, 0)):

@@ -32,12 +32,14 @@ CENTRE_TILES = BANK // P
 CENTRE_HALVES = NCLASS // BANK
 CENTRE_PAIRS = NCLASS // (2 * P)
 
-QUANT_LAG = 1
-PROJECT_LAG = 2
-RELU_LAG = 3
-LAYOUT_LAG = 4
-FEAT_QUANT_LAG = 5
-NORM_LAG = 5
+START = 0
+LEAD = 3
+QUANT_LAG = 2 + START
+PROJECT_LAG = 2 + LEAD + START
+RELU_LAG = 3 + LEAD + START
+LAYOUT_LAG = 4 + LEAD + START
+FEAT_QUANT_LAG = 5 + LEAD + START
+NORM_LAG = 5 + LEAD + START
 
 FLOPS = 2 * BATCH * IN_F * FEAT * VIEWS + 2 * BATCH * D * NCLASS
 
@@ -67,9 +69,10 @@ def tile_qccpn_pa_kernel(
         def load_unit(h, v, pieces):
             x_raw = stream.tile([P, ROW_TILES, IN_F], BF16, tag="x_raw", bufs=10)
             rows = views[v].rearrange("(h p j) k -> h p j k", h=CHUNKS, p=P)
-            n = ROW_TILES // pieces
+            n = IN_F // pieces
             for i in range(pieces):
-                nc.sync.dma_start(out=x_raw[:, i * n : (i + 1) * n, :], in_=rows[h][:, i * n : (i + 1) * n, :])
+                cols = slice(i * n, (i + 1) * n)
+                nc.sync.dma_start(out=x_raw[:, :, cols], in_=rows[h][:, :, cols])
             return x_raw
 
         def load_centre_pair(cp):
@@ -82,7 +85,6 @@ def tile_qccpn_pa_kernel(
         w_raw = [keep.tile([P, IN_PASSES, FEAT], U32, align_bytes=64, name="w_raw%d" % w) for w in range(2)]
         s_raw = [keep.tile([P, FEAT], U8, align_bytes=64, name="s_raw%d" % w) for w in range(2)]
         bias_rows = keep.tile([P, 2 * P], BF16)
-        warm = keep.tile([P, BANK], BF16)
         for w in range(2):
             nc.vector.memset(s_raw[w][:].bitcast(I32), 0)
         nc.vector.memset(bias_rows[:], 0.0)
@@ -103,24 +105,21 @@ def tile_qccpn_pa_kernel(
             for w, bias in enumerate((b_f, b_r)):
                 nc.sync.dma_start(out=bias_rows[2 * w : 2 * w + 2, :], in_=bias.rearrange("(u m) -> u m", u=2))
 
-        x_tiles = [load_unit(*units[0], 2), load_unit(*units[1], 1)]
-        load_weight(0)
-        load_biases()
-        load_weight(1)
-        c_tiles = [load_centre_pair(0)]
-        x_tiles.append(load_unit(*units[2], 1))
-        x_tiles.append(load_unit(*units[3], 1))
-        c_tiles.append(load_centre_pair(1))
-        for h, v in units[4:6]:
-            x_tiles.append(load_unit(h, v, 1))
-        c_tiles.append(load_centre_pair(2))
-        for h, v in units[6:8]:
-            x_tiles.append(load_unit(h, v, 1))
-        c_tiles.append(load_centre_pair(3))
-        for h, v in units[8:]:
-            x_tiles.append(load_unit(h, v, 1))
+        x_tiles, c_tiles = [], []
 
-        nc.vector.tensor_copy(out=warm[:], in_=x_tiles[0][:, 0, 0:BANK])
+        def load(what):
+            for item in what:
+                if item == "f":
+                    load_weight(0)
+                    load_biases()
+                elif item == "r":
+                    load_weight(1)
+                elif item == "c":
+                    c_tiles.append(load_centre_pair(len(c_tiles)))
+                else:
+                    x_tiles.append(load_unit(*units[len(x_tiles)], 2 if len(x_tiles) == 0 else 1))
+
+        load("xxfxrcxcxxxcxcxxxxxxxx")
 
         w_words = keep.tile([P, 2, IN_PASSES, FEAT], U32, align_bytes=64)
         w_scales = keep.tile([P, 2, FEAT], U8, align_bytes=64)
@@ -170,20 +169,20 @@ def tile_qccpn_pa_kernel(
             x_banks[u, g] = xt
 
         def copy_x(u, g):
-            x_grp = stream.tile([P, ROWS, PACK], BF16, tag="x_grp", bufs=3, align_bytes=64)
-            x_groups[u, g] = x_grp
-            nc.vector.tensor_copy(out=x_grp[:].bitcast(F32), in_=x_banks.pop((u, g))[:].rearrange("p e b -> p b e"))
-
-        def quantise_x(u, g):
             if g == 0:
-                x_words = stream.tile([P, IN_PASSES, ROWS], U32, tag="x_words", bufs=3, align_bytes=64)
-                x_scales = stream.tile([P, IN_PASSES, ROWS], U8, tag="x_scales", bufs=3, align_bytes=64)
-                x_operands[u] = (x_words, x_scales)
-            x_words, x_scales = x_operands[u]
+                x_grp = stream.tile([P, IN_PASSES, ROWS, PACK], BF16, tag="x_grp", bufs=3, align_bytes=64)
+                x_groups[u] = x_grp
+            copy = nc.scalar.copy if (u, g) in x_on_scalar else nc.vector.tensor_copy
+            copy(out=x_groups[u][:, g, :, :].bitcast(F32), in_=x_banks.pop((u, g))[:].rearrange("p e b -> p b e"))
+
+        def quantise_x(u):
+            x_words = stream.tile([P, IN_PASSES, ROWS], U32, tag="x_words", bufs=2 + LEAD // 2, align_bytes=64)
+            x_scales = stream.tile([P, IN_PASSES, ROWS], U8, tag="x_scales", bufs=2 + LEAD // 2, align_bytes=64)
+            x_operands[u] = (x_words, x_scales)
             nc.vector.quantize_mx(
-                out=x_words[:, g, :].bitcast(FP8X4),
-                scales=x_scales[:, g, :],
-                in_=x_groups.pop((u, g))[:].rearrange("p b t -> p (b t)"),
+                out=x_words[:].rearrange("p g b -> p (g b)").bitcast(FP8X4),
+                scales=x_scales[:].rearrange("p g b -> p (g b)"),
+                in_=x_groups.pop(u)[:].rearrange("p g b t -> p (g b t)"),
             )
 
         def transpose_c(cp, v):
@@ -198,9 +197,9 @@ def tile_qccpn_pa_kernel(
             c_banks[cp, v] = ct
 
         def copy_c(cp, v):
-            c_grp = stream.tile([P, 2 * P, PACK], BF16, tag="c_grp", align_bytes=64)
+            c_grp = stream.tile([P, 2 * P, PACK], BF16, tag="c_grp", bufs=3, align_bytes=64)
             c_groups[cp, v] = c_grp
-            copy = nc.scalar.copy if cp >= 2 and v % 2 == 1 else nc.vector.tensor_copy
+            copy = nc.vector.tensor_copy if (cp, v) in c_on_vector else nc.scalar.copy
             copy(
                 out=c_grp[:].bitcast(F32),
                 in_=c_banks.pop((cp, v))[:].rearrange("p u c -> p c u"),
@@ -239,14 +238,9 @@ def tile_qccpn_pa_kernel(
         def copy_c2(cp):
             nc.vector.tensor_copy(out=c2_rows[:, 2 * P * cp : 2 * P * (cp + 1)], in_=c_banks.pop(cp)[:])
 
-        def keep_warm(bank, n):
-            nc.tensor.matmul(out=bank, lhsT=warm[:, 0:P], rhs=warm[:, 0:n], start=True, stop=True)
-
-        def project(u, k, extra):
+        def project(u, k):
             w = weight_of_view[units[u][1]]
             acc = psum.tile([P, 2, ROWS], F32, tag="s1", bufs=2)
-            if extra:
-                keep_warm(acc[:].rearrange("p i b -> p (i b)"), BANK)
             for i in range(2):
                 cols = slice((2 * k + i) * P, (2 * k + i + 1) * P)
                 for g in range(IN_PASSES):
@@ -267,7 +261,7 @@ def tile_qccpn_pa_kernel(
                 feat = stream.tile([P, PACK, ROWS], F32, tag="feat", bufs=4)
                 feats[u] = feat
             acc = s1_banks.pop((u, k))
-            for i in range(2):
+            for i in (1, 0):
                 nc.scalar.activation(
                     out=feats[u][:, 2 * k + i, :], in_=acc[:, i, :], func=ACT.Relu, bias=bias_cols[:, w, k, i : i + 1]
                 )
@@ -275,7 +269,10 @@ def tile_qccpn_pa_kernel(
         def lay_out_feat(u):
             f_grp = stream.tile([P, ROWS, PACK], BF16, tag="f_grp", align_bytes=64)
             f_groups[u] = f_grp
-            nc.vector.tensor_copy(out=f_grp[:], in_=feats[u][:].rearrange("p t b -> p b t"))
+            nc.vector.tensor_copy(
+                out=f_grp[:].rearrange("p (b i) t -> p b t i", i=4),
+                in_=feats[u][:].rearrange("p t (b i) -> p b t i", i=4),
+            )
 
         def quantise_feat(u):
             h, v = units[u]
@@ -312,138 +309,146 @@ def tile_qccpn_pa_kernel(
                 out=f2_cols[:, rows], in_=f2_parts[:, rows, :], axis=mybir.AxisListType.X, op=ALU.add
             )
 
-        def score(h, cp):
-            cols = slice(2 * P * cp, 2 * P * (cp + 1))
-            f_words, f_scales = f_operands[h]
-            cross = psum.tile([P, ROW_TILES, 2 * P], F32, tag="tc", bufs=2)
-            for j in range(ROW_TILES):
-                for v in range(VIEWS):
-                    nc.tensor.matmul_mx(
-                        out=cross[:, j, :],
-                        lhsT=f_words[:, v, j * P : (j + 1) * P].bitcast(FP8X4),
-                        lhsT_scale=f_scales[:, v, j * P : (j + 1) * P],
-                        rhs=c_words[:, v, cols].bitcast(FP8X4),
-                        rhs_scale=c_scales[:, v, cols],
-                        start=(v == 0),
-                        stop=(v == VIEWS - 1),
-                    )
-            score_banks[h, cp] = cross
+        def score(c, j, ch):
+            rows = slice(j * P, (j + 1) * P)
+            cols = slice(BANK * ch, BANK * (ch + 1))
+            f_words, f_scales = f_operands[c]
+            cross = psum.tile([P, BANK], F32, tag="tc", bufs=2)
+            for v in range(VIEWS):
+                nc.tensor.matmul_mx(
+                    out=cross[:],
+                    lhsT=f_words[:, v, rows].bitcast(FP8X4),
+                    lhsT_scale=f_scales[:, v, rows],
+                    rhs=c_words[:, v, cols].bitcast(FP8X4),
+                    rhs_scale=c_scales[:, v, cols],
+                    start=(v == 0),
+                    stop=(v == VIEWS - 1),
+                )
+            score_banks[c, j, ch] = cross
 
-        def add_c2(h, cp):
-            d2 = stream.tile([P, ROW_TILES, 2 * P], F32, tag="d2", bufs=4)
+        def add_c2(c, j, ch):
+            d2 = stream.tile([P, BANK], F32, tag="d2", bufs=4)
             nc.vector.scalar_tensor_tensor(
                 out=d2[:],
-                in0=score_banks.pop((h, cp))[:],
+                in0=score_banks.pop((c, j, ch))[:],
                 scalar=-2.0,
-                in1=c2_rows[:, 2 * P * cp : 2 * P * (cp + 1)].unsqueeze(1).to_broadcast([P, ROW_TILES, 2 * P]),
+                in1=c2_rows[:, BANK * ch : BANK * (ch + 1)],
                 op0=ALU.mult,
                 op1=ALU.add,
             )
-            d2_tiles[h, cp] = d2
+            d2_tiles[c, j, ch] = d2
 
-        def add_f2(h, cp):
-            d2 = d2_tiles[h, cp]
-            for j in range(ROW_TILES):
-                row = ROW_TILES * h + j
-                nc.vector.tensor_scalar(
-                    out=d2[:, j, :],
-                    in0=d2[:, j, :],
-                    scalar1=f2_cols[:, row : row + 1],
-                    scalar2=0.0,
-                    op0=ALU.add,
-                    op1=ALU.max,
-                )
+        def add_f2(c, j, ch):
+            d2 = d2_tiles[c, j, ch]
+            row = ROW_TILES * c + j
+            nc.vector.tensor_scalar(
+                out=d2[:], in0=d2[:], scalar1=f2_cols[:, row : row + 1], scalar2=0.0, op0=ALU.add, op1=ALU.max
+            )
 
-        def root(h, cp):
-            dist = stream.tile([P, ROW_TILES, 2 * P], F32, tag="dist", bufs=4)
-            nc.scalar.activation(out=dist[:], in_=d2_tiles.pop((h, cp))[:], func=ACT.Sqrt)
-            dist_tiles[h, cp] = dist
+        def root(c, j, ch):
+            dist = stream.tile([P, BANK], F32, tag="dist", bufs=4)
+            nc.scalar.activation(out=dist[:], in_=d2_tiles.pop((c, j, ch))[:], func=ACT.Sqrt)
+            dist_tiles[c, j, ch] = dist
 
-        def store(h, cp):
-            scores = stream.tile([P, ROW_TILES, 2 * P], F32, tag="scores", bufs=4)
-            nc.vector.tensor_scalar_mul(out=scores[:], in0=dist_tiles.pop((h, cp))[:], scalar1=-GAMMA)
-            out_rows = out.rearrange("(h p j) c -> h p j c", h=CHUNKS, p=P)
-            nc.sync.dma_start(out=out_rows[h][:, :, 2 * P * cp : 2 * P * (cp + 1)], in_=scores[:])
+        def store(c, j, ch):
+            scores = stream.tile([P, BANK], F32, tag="scores", bufs=4)
+            nc.vector.tensor_scalar_mul(out=scores[:], in0=dist_tiles.pop((c, j, ch))[:], scalar1=-GAMMA)
+            out_rows = out.rearrange("(h p j) c -> h j p c", h=CHUNKS, p=P)
+            nc.sync.dma_start(out=out_rows[c, j][:, BANK * ch : BANK * (ch + 1)], in_=scores[:])
 
         def part_of(step, lag):
             k = step - lag
             return divmod(k, PARTS) if 0 <= k < UNITS * PARTS else None
 
-        centre_at = [3, 4, 5, 7, 8, 9, 11, 12, 13, 15, 16, 18, 20, 22, 24, 26]
-        centre_jobs = {s: divmod(k, VIEWS) for k, s in enumerate(centre_at)}
-        square_at = [3, 4, 5, 7, 8, 9, 11, 12, 13, 15, 16, 18, 20, 22, 24, 26]
-        square_jobs = {s: divmod(k, 2) for k, s in enumerate(square_at)}
-        c2_steps = {8: 0, 13: 1, 19: 2, 27: 3}
-        score_order = [(0, 0), (0, 1), (0, 2), (1, 0), (1, 1), (1, 2), (0, 3), (1, 3), (2, 0), (2, 1), (2, 2), (2, 3), (3, 0), (3, 1), (3, 2), (3, 3)]
-        score_at = [13, 15, 20, 22, 24, 26, 28, 29, 30, 31, 33, 34, 36, 37, 38, 39]
-        score_steps = dict(zip(score_at, score_order))
+        c_on_vector = [(a, b) for a in range(4) for b in (0, 1, 2)]
+        x_on_scalar = [(0, 1), (1, 1)]
+        w_steps = (3, 4)
+        centre_at = list(range(6, 14)) + list(range(14, 30, 2))
+        square_at = [s - 1 for s in centre_at]
+        score_order = [(c, j, ch) for c, ch in ((0, 0), (1, 0), (0, 1), (1, 1), (2, 0), (2, 1), (3, 0), (3, 1)) for j in range(ROW_TILES)]
+        score_at = [20, 22, 24, 26, 31, 31, 32, 33, 34, 35, 37, 37, 38, 39, 40, 41]
+        tail = 37
+        centre_jobs = {}
+        for k, s in enumerate(centre_at):
+            centre_jobs.setdefault(s, []).append(divmod(k, VIEWS))
+        square_jobs, c2_steps, sum2_steps = {}, {}, {}
+        for k, sq in enumerate(square_at):
+            square_jobs.setdefault(sq, []).append(divmod(k, 2))
+            if k % 4 == 3:
+                sum2_steps[sq + 1] = k // 4
+                c2_steps[sq + 3] = k // 4
+        score_steps = {}
+        for s, group in zip(score_at, score_order):
+            score_steps.setdefault(s, []).append(group)
+        norm_steps, sum_steps = {}, {}
+        for u in range(UNITS):
+            for j in range(ROW_TILES):
+                s = PARTS * u + NORM_LAG + (j if u < UNITS - 1 else 0)
+                norm_steps.setdefault(s, []).append((u, j))
+                if units[u][1] == VIEWS - 1 and j == ROW_TILES - 1:
+                    sum_steps[s + 1] = units[u][0]
+        root_steps, store_steps = {}, {}
+        for s, group in zip(score_at, score_order):
+            root_steps.setdefault(s + (1 if s >= tail else 2), []).append(group)
+            store_steps.setdefault(s + (2 if s >= tail else 3), []).append(group)
 
-        warm_at = list(range(2, 13)) + list(range(16, 20))
-        warm_head = {0: 0, 1: 3, 2: 5, 3: 1, 4: 1, 5: 1, 6: 1}
-
-        for step in range(45):
-            for i in range(warm_head.get(step, 0)):
-                idle = psum.tile([P, BANK], F32, tag="tc", bufs=2)
-                keep_warm(idle[:], BANK)
-            norm = part_of(step, NORM_LAG)
-            if norm:
+        for step in range(60):
+            for norm in norm_steps.get(step, []):
                 transpose_feat(*norm)
-            xs = part_of(step, 0)
+            xs = part_of(step, START)
             if xs:
                 transpose_x(*xs)
-            if step in centre_jobs:
-                transpose_c(*centre_jobs[step])
-            if step - 1 in c2_steps:
-                transpose_c2(c2_steps[step - 1])
+            for job in centre_jobs.get(step, []):
+                transpose_c(*job)
+            if step in c2_steps:
+                transpose_c2(c2_steps[step])
 
             rel = part_of(step, RELU_LAG)
             if rel:
                 relu(*rel)
-            if step - 1 in score_steps:
-                add_c2(*score_steps[step - 1])
             fq = part_of(step, FEAT_QUANT_LAG)
             if fq and fq[1] == 0:
                 quantise_feat(fq[0])
-            xq = part_of(step, QUANT_LAG)
-            if xq:
-                quantise_x(*xq)
+            for group in score_steps.get(step - 1, []):
+                add_c2(*group)
+            for job in centre_jobs.get(step, []):
+                copy_c(*job)
             if xs:
                 copy_x(*xs)
-            if norm:
+            for norm in norm_steps.get(step, []):
                 square_feat(*norm)
-            if step in centre_jobs:
-                copy_c(*centre_jobs[step])
-            if step - 1 in c2_steps:
-                copy_c2(c2_steps[step - 1])
-            summed = part_of(step, NORM_LAG + 1)
-            if summed and units[summed[0]][1] == VIEWS - 1 and summed[1] == ROW_TILES - 1:
-                sum_f2(units[summed[0]][0])
-            if step - 1 in score_steps:
-                add_f2(*score_steps[step - 1])
-            if step - 1 in centre_jobs:
-                quantise_c(*centre_jobs[step - 1])
-            if step == 1:
+            if step in c2_steps:
+                copy_c2(c2_steps[step])
+            xq = part_of(step, QUANT_LAG)
+            if xq and xq[1] == 0:
+                quantise_x(xq[0])
+            if step in sum_steps:
+                sum_f2(sum_steps[step])
+            for job in centre_jobs.get(step - 1, []):
+                quantise_c(*job)
+            for group in score_steps.get(step - 1, []):
+                add_f2(*group)
+            if step == w_steps[0]:
                 permute_weight(0, 0)
-            if step == 2:
                 permute_weight(0, 1)
                 spread_bias()
-            if step == 3:
+            if step == w_steps[1]:
                 permute_weight(1, 0)
                 permute_weight(1, 1)
-            if step in square_jobs:
-                square_c(*square_jobs[step])
-            if step - 2 in score_steps:
-                root(*score_steps[step - 2])
+            for job in square_jobs.get(step, []):
+                square_c(*job)
+            if step in sum2_steps:
+                sum_c2(sum2_steps[step])
+            for group in root_steps.get(step, []):
+                root(*group)
             lay = part_of(step, LAYOUT_LAG)
             if lay and lay[1] == 0:
                 lay_out_feat(lay[0])
-            if step - 3 in score_steps:
-                store(*score_steps[step - 3])
-            if step in c2_steps:
-                sum_c2(c2_steps[step])
+            for group in store_steps.get(step, []):
+                store(*group)
 
             proj = part_of(step, PROJECT_LAG)
             if proj:
-                project(*proj, step in warm_at)
-            if step in score_steps:
-                score(*score_steps[step])
+                project(*proj)
+            for group in score_steps.get(step, []):
+                score(*group)

@@ -1,3 +1,4 @@
+import math
 from contextlib import ExitStack
 
 import concourse.mybir as mybir
@@ -64,7 +65,9 @@ def tile_qccpn_pa_kernel(
         one = keep.tile([P, 1], F32)
         nc.vector.memset(one[:], 1.0)
         root_of_one = keep.tile([P, 1], F32)
-        nc.scalar.activation(out=root_of_one[:], in_=one[:], func=ACT.Sqrt)
+        nc.scalar.activation(out=root_of_one[:], in_=one[:], func=ACT.Abs_reciprocal_sqrt)
+        tiny = keep.tile([P, 1], F32)
+        nc.vector.memset(tiny[:], 1e-30)
 
         def load_unit(h, v, pieces):
             x_raw = stream.tile([P, ROW_TILES, IN_F], BF16, tag="x_raw", bufs=10)
@@ -119,7 +122,7 @@ def tile_qccpn_pa_kernel(
                 else:
                     x_tiles.append(load_unit(*units[len(x_tiles)], 2 if len(x_tiles) == 0 else 1))
 
-        load("xxfxrcxcxxxcxcxxxxxxxx")
+        load("xxxcfxrccxcxxxxxxxxxxx")
 
         w_words = keep.tile([P, 2, IN_PASSES, FEAT], U32, align_bytes=64)
         w_scales = keep.tile([P, 2, FEAT], U8, align_bytes=64)
@@ -154,7 +157,7 @@ def tile_qccpn_pa_kernel(
         x_banks, x_groups, x_operands = {}, {}, {}
         c_banks, c_groups = {}, {}
         s1_banks, feats, f_groups, f_banks, f_operands = {}, {}, {}, {}, {}
-        score_banks, d2_tiles, dist_tiles = {}, {}, {}
+        score_banks, half_tiles, root_tiles = {}, {}, {}
 
         def transpose_x(u, g):
             xt = psum.tile([P, 2, ROWS], F32, tag="tx", bufs=2)
@@ -219,6 +222,7 @@ def tile_qccpn_pa_kernel(
                 out=c_sq[:],
                 in_=c_tiles[i // 2][:, i % 2, half * (D // 2) : (half + 1) * (D // 2)],
                 func=ACT.Square,
+                scale=math.sqrt(0.5),
                 accum_out=c2_parts[:, i, half : half + 1],
             )
 
@@ -300,6 +304,7 @@ def tile_qccpn_pa_kernel(
                 out=f_sq[:],
                 in_=f_banks.pop((u, j))[:],
                 func=ACT.Square,
+                scale=math.sqrt(0.5),
                 accum_out=f2_parts[:, ROW_TILES * h + j, v : v + 1],
             )
 
@@ -309,11 +314,11 @@ def tile_qccpn_pa_kernel(
                 out=f2_cols[:, rows], in_=f2_parts[:, rows, :], axis=mybir.AxisListType.X, op=ALU.add
             )
 
-        def score(c, j, ch):
+        def score(c, j, first, width):
             rows = slice(j * P, (j + 1) * P)
-            cols = slice(BANK * ch, BANK * (ch + 1))
+            cols = slice(first, first + width)
             f_words, f_scales = f_operands[c]
-            cross = psum.tile([P, BANK], F32, tag="tc", bufs=2)
+            cross = psum.tile([P, width], F32, tag="tc", bufs=2)
             for v in range(VIEWS):
                 nc.tensor.matmul_mx(
                     out=cross[:],
@@ -324,50 +329,58 @@ def tile_qccpn_pa_kernel(
                     start=(v == 0),
                     stop=(v == VIEWS - 1),
                 )
-            score_banks[c, j, ch] = cross
+            score_banks[c, j, first] = cross
 
-        def add_c2(c, j, ch):
-            d2 = stream.tile([P, BANK], F32, tag="d2", bufs=4)
-            nc.vector.scalar_tensor_tensor(
-                out=d2[:],
-                in0=score_banks.pop((c, j, ch))[:],
-                scalar=-2.0,
-                in1=c2_rows[:, BANK * ch : BANK * (ch + 1)],
-                op0=ALU.mult,
-                op1=ALU.add,
-            )
-            d2_tiles[c, j, ch] = d2
-
-        def add_f2(c, j, ch):
-            d2 = d2_tiles[c, j, ch]
+        def take_score(c, j, first, width):
             row = ROW_TILES * c + j
-            nc.vector.tensor_scalar(
-                out=d2[:], in0=d2[:], scalar1=f2_cols[:, row : row + 1], scalar2=0.0, op0=ALU.add, op1=ALU.max
+            half = stream.tile([P, width], F32, tag="half", bufs=4)
+            nc.vector.scalar_tensor_tensor(
+                out=half[:],
+                in0=score_banks.pop((c, j, first))[:],
+                scalar=f2_cols[:, row : row + 1],
+                in1=c2_rows[:, first : first + width],
+                op0=ALU.subtract,
+                op1=ALU.subtract,
             )
+            half_tiles[c, j, first] = half
 
-        def root(c, j, ch):
-            dist = stream.tile([P, BANK], F32, tag="dist", bufs=4)
-            nc.scalar.activation(out=dist[:], in_=d2_tiles.pop((c, j, ch))[:], func=ACT.Sqrt)
-            dist_tiles[c, j, ch] = dist
+        def root(c, j, first, width):
+            r = stream.tile([P, width], F32, tag="r", bufs=4)
+            nc.scalar.activation(
+                out=r[:],
+                in_=half_tiles[c, j, first][:],
+                func=ACT.Abs_reciprocal_sqrt,
+                scale=0.5 / GAMMA**2,
+                bias=tiny[:],
+            )
+            root_tiles[c, j, first] = r
 
-        def store(c, j, ch):
-            scores = stream.tile([P, BANK], F32, tag="scores", bufs=4)
-            nc.vector.tensor_scalar_mul(out=scores[:], in0=dist_tiles.pop((c, j, ch))[:], scalar1=-GAMMA)
+        def store(c, j, first, width):
+            scores = stream.tile([P, width], F32, tag="scores", bufs=4)
+            nc.vector.scalar_tensor_tensor(
+                out=scores[:],
+                in0=half_tiles.pop((c, j, first))[:],
+                scalar=0.0,
+                in1=root_tiles.pop((c, j, first))[:],
+                op0=ALU.min,
+                op1=ALU.mult,
+            )
             out_rows = out.rearrange("(h p j) c -> h j p c", h=CHUNKS, p=P)
-            nc.sync.dma_start(out=out_rows[c, j][:, BANK * ch : BANK * (ch + 1)], in_=scores[:])
+            nc.sync.dma_start(out=out_rows[c, j][:, first : first + width], in_=scores[:])
 
         def part_of(step, lag):
             k = step - lag
             return divmod(k, PARTS) if 0 <= k < UNITS * PARTS else None
 
-        c_on_vector = [(a, b) for a in range(4) for b in (0, 1, 2)]
-        x_on_scalar = [(0, 1), (1, 1)]
-        w_steps = (3, 4)
-        centre_at = list(range(6, 14)) + list(range(14, 30, 2))
-        square_at = [s - 1 for s in centre_at]
-        score_order = [(c, j, ch) for c, ch in ((0, 0), (1, 0), (0, 1), (1, 1), (2, 0), (2, 1), (3, 0), (3, 1)) for j in range(ROW_TILES)]
-        score_at = [20, 22, 24, 26, 31, 31, 32, 33, 34, 35, 37, 37, 38, 39, 40, 41]
+        last_split = 2
+        doubled_from = 16
         tail = 37
+        c_on_vector = [(a, b) for a in range(4) for b in (0, 1, 2)]
+        w_steps = (4, 5)
+        score_at = [20, 22, 24, 26, 29, 30, 31, 32, 33, 34, 36, 37, 38, 39, 40, 41]
+        x_on_scalar = [(0, 1), (1, 1)] + [(u, 0) for u in range(3, 16, 4)]
+        centre_at = [4, 5, 6, 7] + list(range(8, 12)) + list(range(12, 28, 2))
+        square_at = [3, 4, 5, 6] + list(range(7, 11)) + list(range(11, 27, 2))
         centre_jobs = {}
         for k, s in enumerate(centre_at):
             centre_jobs.setdefault(s, []).append(divmod(k, VIEWS))
@@ -377,9 +390,15 @@ def tile_qccpn_pa_kernel(
             if k % 4 == 3:
                 sum2_steps[sq + 1] = k // 4
                 c2_steps[sq + 3] = k // 4
+        score_order = []
+        for c, ch in ((0, 0), (1, 0), (0, 1), (1, 1), (2, 0), (2, 1), (3, 0), (3, 1)):
+            for j in range(ROW_TILES):
+                score_order.append([(c, j, BANK * ch, BANK)])
+        c, j, first, width = score_order[-1][0]
+        score_order[-1] = [(c, j, first + k * width // last_split, width // last_split) for k in range(last_split)]
         score_steps = {}
         for s, group in zip(score_at, score_order):
-            score_steps.setdefault(s, []).append(group)
+            score_steps.setdefault(s, []).extend(group)
         norm_steps, sum_steps = {}, {}
         for u in range(UNITS):
             for j in range(ROW_TILES):
@@ -387,12 +406,15 @@ def tile_qccpn_pa_kernel(
                 norm_steps.setdefault(s, []).append((u, j))
                 if units[u][1] == VIEWS - 1 and j == ROW_TILES - 1:
                     sum_steps[s + 1] = units[u][0]
-        root_steps, store_steps = {}, {}
+        summed = {c: s for s, c in sum_steps.items()}
+        take_steps, root_steps, store_steps = {}, {}, {}
         for s, group in zip(score_at, score_order):
-            root_steps.setdefault(s + (1 if s >= tail else 2), []).append(group)
-            store_steps.setdefault(s + (2 if s >= tail else 3), []).append(group)
+            f = max(s + 1, summed[group[0][0]])
+            take_steps.setdefault(f, []).extend(group)
+            root_steps.setdefault(f + (0 if s >= tail else 1), []).extend(group)
+            store_steps.setdefault(f + (1 if s >= tail else 2), []).extend(group)
 
-        for step in range(60):
+        def transposes(step):
             for norm in norm_steps.get(step, []):
                 transpose_feat(*norm)
             xs = part_of(step, START)
@@ -403,14 +425,19 @@ def tile_qccpn_pa_kernel(
             if step in c2_steps:
                 transpose_c2(c2_steps[step])
 
+        transposes(0)
+        for step in range(60):
+            xs = part_of(step, START)
             rel = part_of(step, RELU_LAG)
             if rel:
                 relu(*rel)
             fq = part_of(step, FEAT_QUANT_LAG)
             if fq and fq[1] == 0:
                 quantise_feat(fq[0])
-            for group in score_steps.get(step - 1, []):
-                add_c2(*group)
+            if step in sum_steps:
+                sum_f2(sum_steps[step])
+            for group in take_steps.get(step, []):
+                take_score(*group)
             for job in centre_jobs.get(step, []):
                 copy_c(*job)
             if xs:
@@ -422,12 +449,8 @@ def tile_qccpn_pa_kernel(
             xq = part_of(step, QUANT_LAG)
             if xq and xq[1] == 0:
                 quantise_x(xq[0])
-            if step in sum_steps:
-                sum_f2(sum_steps[step])
             for job in centre_jobs.get(step - 1, []):
                 quantise_c(*job)
-            for group in score_steps.get(step - 1, []):
-                add_f2(*group)
             if step == w_steps[0]:
                 permute_weight(0, 0)
                 permute_weight(0, 1)
@@ -447,8 +470,13 @@ def tile_qccpn_pa_kernel(
             for group in store_steps.get(step, []):
                 store(*group)
 
+            early = step >= doubled_from and step % 2 == 0
+            if early:
+                transposes(step + 1)
             proj = part_of(step, PROJECT_LAG)
             if proj:
                 project(*proj)
             for group in score_steps.get(step, []):
                 score(*group)
+            if not early:
+                transposes(step + 1)

@@ -122,7 +122,7 @@ def tile_qccpn_pa_kernel(
                 else:
                     x_tiles.append(load_unit(*units[len(x_tiles)], 2 if len(x_tiles) == 0 else 1))
 
-        load("xxxcfxrccxcxxxxxxxxxxx")
+        load("xxxcfxrcxcxcxxxxxxxxxx")
 
         w_words = keep.tile([P, 2, IN_PASSES, FEAT], U32, align_bytes=64)
         w_scales = keep.tile([P, 2, FEAT], U8, align_bytes=64)

@@ -15,7 +15,6 @@ ALU = mybir.AluOpType
 
 P = 128
 PACK = 4
-K_PASS = P * PACK
 BANK = 512
 
 BATCH, IN_F, FEAT, NCLASS = 1024, 1024, 512, 1024
@@ -23,24 +22,22 @@ VIEWS = 4
 D = VIEWS * FEAT
 GAMMA = 0.1
 
+IN_PASSES = IN_F // (P * PACK)
 ROWS = 256
 CHUNKS = BATCH // ROWS
 ROW_TILES = ROWS // P
-IN_PASSES = IN_F // K_PASS
 UNITS = CHUNKS * VIEWS
 PARTS = 2
-CENTRE_TILES = BANK // P
-CENTRE_HALVES = NCLASS // BANK
-CENTRE_PAIRS = NCLASS // (2 * P)
+PAIR = 2 * P
+CENTRE_PAIRS = NCLASS // PAIR
+CENTRE_JOBS = CENTRE_PAIRS * VIEWS
 
-START = 0
-LEAD = 3
-QUANT_LAG = 2 + START
-PROJECT_LAG = 2 + LEAD + START
-RELU_LAG = 3 + LEAD + START
-LAYOUT_LAG = 4 + LEAD + START
-FEAT_QUANT_LAG = 5 + LEAD + START
-NORM_LAG = 5 + LEAD + START
+QUANT_LAG = 2
+PROJECT_LAG = 5
+RELU_LAG = PROJECT_LAG + 1
+LAYOUT_LAG = PROJECT_LAG + 2
+FEAT_LAG = PROJECT_LAG + 3
+X_STEPS = UNITS * PARTS
 
 FLOPS = 2 * BATCH * IN_F * FEAT * VIEWS + 2 * BATCH * D * NCLASS
 
@@ -50,8 +47,9 @@ def tile_qccpn_pa_kernel(
 ):
     nc = tc.nc
     views = [x, x_90, x_180, x_270]
+    weights = [(W_f_words, W_f_scales), (W_r_words, W_r_scales)]
     weight_of_view = [0, 1, 1, 1]
-    units = [(h, v) for h in range(CHUNKS) for v in range(VIEWS)]
+    units = [(chunk, v) for chunk in range(CHUNKS) for v in range(VIEWS)]
 
     with ExitStack() as stack:
         keep = stack.enter_context(tc.tile_pool(name="keep", bufs=1))
@@ -69,21 +67,23 @@ def tile_qccpn_pa_kernel(
         tiny = keep.tile([P, 1], F32)
         nc.vector.memset(tiny[:], 1e-30)
 
-        def load_unit(h, v, pieces):
-            x_raw = stream.tile([P, ROW_TILES, IN_F], BF16, tag="x_raw", bufs=10)
-            rows = views[v].rearrange("(h p j) k -> h p j k", h=CHUNKS, p=P)
-            n = IN_F // pieces
-            for i in range(pieces):
-                cols = slice(i * n, (i + 1) * n)
-                nc.sync.dma_start(out=x_raw[:, :, cols], in_=rows[h][:, :, cols])
-            return x_raw
+        x_tiles, c_tiles = [], []
 
-        def load_centre_pair(cp):
+        def load_x(pieces=1):
+            chunk, v = units[len(x_tiles)]
+            x_raw = stream.tile([P, ROW_TILES, IN_F], BF16, tag="x_raw", bufs=10)
+            rows = views[v].rearrange("(c p j) k -> c p j k", c=CHUNKS, p=P)
+            for i in range(pieces):
+                cols = slice(i * IN_F // pieces, (i + 1) * IN_F // pieces)
+                nc.sync.dma_start(out=x_raw[:, :, cols], in_=rows[chunk][:, :, cols])
+            x_tiles.append(x_raw)
+
+        def load_centres():
             c_raw = stream.tile([P, 2, D], BF16, tag="c_raw", bufs=CENTRE_PAIRS)
             rows = centers.rearrange("(cp i p) k -> cp i p k", cp=CENTRE_PAIRS, p=P)
             for i in range(2):
-                nc.sync.dma_start(out=c_raw[:, i, :], in_=rows[cp, i])
-            return c_raw
+                nc.sync.dma_start(out=c_raw[:, i, :], in_=rows[len(c_tiles), i])
+            c_tiles.append(c_raw)
 
         w_raw = [keep.tile([P, IN_PASSES, FEAT], U32, align_bytes=64, name="w_raw%d" % w) for w in range(2)]
         s_raw = [keep.tile([P, FEAT], U8, align_bytes=64, name="s_raw%d" % w) for w in range(2)]
@@ -93,10 +93,9 @@ def tile_qccpn_pa_kernel(
         nc.vector.memset(bias_rows[:], 0.0)
 
         def load_weight(w):
-            words, scales = ((W_f_words, W_f_scales), (W_r_words, W_r_scales))[w]
+            words, scales = weights[w]
             nc.sync.dma_start(
-                out=w_raw[w][:].bitcast(I32),
-                in_=words.rearrange("g p n t -> p g (n t)").bitcast(I32),
+                out=w_raw[w][:].bitcast(I32), in_=words.rearrange("g p n t -> p g (n t)").bitcast(I32)
             )
             for quadrant in range(4):
                 nc.sync.dma_start(
@@ -108,43 +107,23 @@ def tile_qccpn_pa_kernel(
             for w, bias in enumerate((b_f, b_r)):
                 nc.sync.dma_start(out=bias_rows[2 * w : 2 * w + 2, :], in_=bias.rearrange("(u m) -> u m", u=2))
 
-        x_tiles, c_tiles = [], []
-
-        def load(what):
-            for item in what:
-                if item == "f":
-                    load_weight(0)
-                    load_biases()
-                elif item == "r":
-                    load_weight(1)
-                elif item == "c":
-                    c_tiles.append(load_centre_pair(len(c_tiles)))
-                else:
-                    x_tiles.append(load_unit(*units[len(x_tiles)], 2 if len(x_tiles) == 0 else 1))
-
-        load("xxxcfxrcxcxcxxxxxxxxxx")
+        load_x(pieces=2)
+        load_x()
+        load_x()
+        load_centres()
+        load_weight(0)
+        load_biases()
+        load_x()
+        load_weight(1)
+        for i in range(CENTRE_PAIRS - 1):
+            load_centres()
+            load_x()
+        for u in range(len(x_tiles), UNITS):
+            load_x()
 
         w_words = keep.tile([P, 2, IN_PASSES, FEAT], U32, align_bytes=64)
         w_scales = keep.tile([P, 2, FEAT], U8, align_bytes=64)
         bias_cols = keep.tile([P, 2, 2, 2], F32)
-
-        def permute_weight(w, u):
-            cols = slice(2 * P * u, 2 * P * (u + 1))
-            nc.vector.tensor_copy(
-                out=w_words[:, w, :, cols].bitcast(I32).rearrange("p g (e m) -> p g e m", e=2),
-                in_=w_raw[w][:, :, cols].bitcast(I32).rearrange("p g (m e) -> p g e m", e=2),
-            )
-            nc.vector.tensor_copy(
-                out=w_scales[:, w, cols].rearrange("p (e m) -> p e m", e=2),
-                in_=s_raw[w][:, cols].rearrange("p (m e) -> p e m", e=2),
-            )
-
-        def spread_bias():
-            bias_ps = psum.tile([P, P], F32, tag="tc", bufs=2)
-            nc.tensor.transpose(bias_ps[:], bias_rows[:].bitcast(F32), ident_f32[:])
-            nc.vector.tensor_copy(
-                out=bias_cols[:].rearrange("p w u e -> p (w u e)"), in_=bias_ps[:].bitcast(BF16)[:, 0:8]
-            )
 
         c_words = keep.tile([P, VIEWS, NCLASS], U32, align_bytes=64)
         c_scales = keep.tile([P, VIEWS, NCLASS], U8, align_bytes=64)
@@ -156,8 +135,27 @@ def tile_qccpn_pa_kernel(
 
         x_banks, x_groups, x_operands = {}, {}, {}
         c_banks, c_groups = {}, {}
-        s1_banks, feats, f_groups, f_banks, f_operands = {}, {}, {}, {}, {}
+        feat_banks, feats, f_groups, f_banks, f_operands = {}, {}, {}, {}, {}
         score_banks, half_tiles, root_tiles = {}, {}, {}
+
+        def permute_weight(w):
+            for u in range(2):
+                cols = slice(2 * P * u, 2 * P * (u + 1))
+                nc.vector.tensor_copy(
+                    out=w_words[:, w, :, cols].bitcast(I32).rearrange("p g (e m) -> p g e m", e=2),
+                    in_=w_raw[w][:, :, cols].bitcast(I32).rearrange("p g (m e) -> p g e m", e=2),
+                )
+                nc.vector.tensor_copy(
+                    out=w_scales[:, w, cols].rearrange("p (e m) -> p e m", e=2),
+                    in_=s_raw[w][:, cols].rearrange("p (m e) -> p e m", e=2),
+                )
+
+        def spread_bias():
+            bias_ps = psum.tile([P, P], F32, tag="tc", bufs=2)
+            nc.tensor.transpose(bias_ps[:], bias_rows[:].bitcast(F32), ident_f32[:])
+            nc.vector.tensor_copy(
+                out=bias_cols[:].rearrange("p w u e -> p (w u e)"), in_=bias_ps[:].bitcast(BF16)[:, 0:8]
+            )
 
         def transpose_x(u, g):
             xt = psum.tile([P, 2, ROWS], F32, tag="tx", bufs=2)
@@ -165,9 +163,7 @@ def tile_qccpn_pa_kernel(
                 words = x_tiles[u][:, j, :].bitcast(F32)
                 for e in range(2):
                     nc.tensor.transpose(
-                        xt[:, e, j * P : (j + 1) * P],
-                        words[:, 256 * g + e : 256 * (g + 1) : 2],
-                        ident_f32[:],
+                        xt[:, e, j * P : (j + 1) * P], words[:, 256 * g + e : 256 * (g + 1) : 2], ident_f32[:]
                     )
             x_banks[u, g] = xt
 
@@ -175,12 +171,13 @@ def tile_qccpn_pa_kernel(
             if g == 0:
                 x_grp = stream.tile([P, IN_PASSES, ROWS, PACK], BF16, tag="x_grp", bufs=3, align_bytes=64)
                 x_groups[u] = x_grp
-            copy = nc.scalar.copy if (u, g) in x_on_scalar else nc.vector.tensor_copy
+            on_scalar = (g == 1 and u < 2) or (g == 0 and u % 4 == 3)
+            copy = nc.scalar.copy if on_scalar else nc.vector.tensor_copy
             copy(out=x_groups[u][:, g, :, :].bitcast(F32), in_=x_banks.pop((u, g))[:].rearrange("p e b -> p b e"))
 
         def quantise_x(u):
-            x_words = stream.tile([P, IN_PASSES, ROWS], U32, tag="x_words", bufs=2 + LEAD // 2, align_bytes=64)
-            x_scales = stream.tile([P, IN_PASSES, ROWS], U8, tag="x_scales", bufs=2 + LEAD // 2, align_bytes=64)
+            x_words = stream.tile([P, IN_PASSES, ROWS], U32, tag="x_words", bufs=3, align_bytes=64)
+            x_scales = stream.tile([P, IN_PASSES, ROWS], U8, tag="x_scales", bufs=3, align_bytes=64)
             x_operands[u] = (x_words, x_scales)
             nc.vector.quantize_mx(
                 out=x_words[:].rearrange("p g b -> p (g b)").bitcast(FP8X4),
@@ -188,28 +185,98 @@ def tile_qccpn_pa_kernel(
                 in_=x_groups.pop(u)[:].rearrange("p g b t -> p (g b t)"),
             )
 
+        def project(u, k):
+            w = weight_of_view[units[u][1]]
+            x_words, x_scales = x_operands[u]
+            acc = psum.tile([P, 2, ROWS], F32, tag="s1", bufs=2)
+            for i in range(2):
+                cols = slice((2 * k + i) * P, (2 * k + i + 1) * P)
+                for g in range(IN_PASSES):
+                    nc.tensor.matmul_mx(
+                        out=acc[:, i, :],
+                        lhsT=w_words[:, w, g, cols].bitcast(FP8X4),
+                        lhsT_scale=w_scales[4 * g : P, w, cols],
+                        rhs=x_words[:, g, :].bitcast(FP8X4),
+                        rhs_scale=x_scales[:, g, :],
+                        start=(g == 0),
+                        stop=(g == IN_PASSES - 1),
+                    )
+            feat_banks[u, k] = acc
+
+        def relu(u, k):
+            w = weight_of_view[units[u][1]]
+            if k == 0:
+                feat = stream.tile([P, PACK, ROWS], F32, tag="feat", bufs=4)
+                feats[u] = feat
+            acc = feat_banks.pop((u, k))
+            for i in (1, 0):
+                nc.scalar.activation(
+                    out=feats[u][:, 2 * k + i, :], in_=acc[:, i, :], func=ACT.Relu, bias=bias_cols[:, w, k, i : i + 1]
+                )
+
+        def lay_out_feat(u):
+            f_grp = stream.tile([P, ROWS, PACK], BF16, tag="f_grp", align_bytes=64)
+            f_groups[u] = f_grp
+            nc.vector.tensor_copy(
+                out=f_grp[:].rearrange("p (b i) t -> p b t i", i=4),
+                in_=feats[u][:].rearrange("p t (b i) -> p b t i", i=4),
+            )
+
+        def quantise_feat(u):
+            chunk, v = units[u]
+            if v == 0:
+                f_words = stream.tile([P, VIEWS, ROWS], U32, tag="f_words", bufs=CHUNKS, align_bytes=64)
+                f_scales = stream.tile([P, VIEWS, ROWS], U8, tag="f_scales", bufs=CHUNKS, align_bytes=64)
+                f_operands[chunk] = (f_words, f_scales)
+            f_words, f_scales = f_operands[chunk]
+            nc.vector.quantize_mx(
+                out=f_words[:, v, :].bitcast(FP8X4),
+                scales=f_scales[:, v, :],
+                in_=f_groups.pop(u)[:].rearrange("p b t -> p (b t)"),
+            )
+
+        def transpose_feat(u, j):
+            ft = psum.tile([P, BANK], F32, tag="tf", bufs=2)
+            for t in range(PACK):
+                nc.tensor.transpose(ft[:, t * P : (t + 1) * P], feats[u][:, t, j * P : (j + 1) * P], ident_f32[:])
+            f_banks[u, j] = ft
+
+        def square_feat(u, j):
+            chunk, v = units[u]
+            f_sq = stream.tile([P, BANK], BF16, tag="f_sq")
+            nc.scalar.activation(
+                out=f_sq[:],
+                in_=f_banks.pop((u, j))[:],
+                func=ACT.Square,
+                scale=math.sqrt(0.5),
+                accum_out=f2_parts[:, ROW_TILES * chunk + j, v : v + 1],
+            )
+
+        def sum_f2(chunk):
+            rows = slice(ROW_TILES * chunk, ROW_TILES * (chunk + 1))
+            nc.vector.tensor_reduce(
+                out=f2_cols[:, rows], in_=f2_parts[:, rows, :], axis=mybir.AxisListType.X, op=ALU.add
+            )
+
         def transpose_c(cp, v):
-            ct = psum.tile([P, 2, 2 * P], F32, tag="tc", bufs=2)
+            ct = psum.tile([P, 2, PAIR], F32, tag="tc", bufs=2)
             for i in range(2):
                 words = c_tiles[cp][:, i, :].bitcast(F32)
                 for u in range(2):
                     first = 256 * v + P * u
-                    nc.tensor.transpose(
-                        ct[:, u, i * P : (i + 1) * P], words[:, first : first + P], ident_f32[:]
-                    )
+                    nc.tensor.transpose(ct[:, u, i * P : (i + 1) * P], words[:, first : first + P], ident_f32[:])
             c_banks[cp, v] = ct
 
         def copy_c(cp, v):
-            c_grp = stream.tile([P, 2 * P, PACK], BF16, tag="c_grp", bufs=3, align_bytes=64)
+            job = VIEWS * cp + v
+            on_scalar = job < 2 * VIEWS and job % 3 == 0
+            c_grp = stream.tile([P, PAIR, PACK], BF16, tag="c_grp", bufs=3, align_bytes=64)
             c_groups[cp, v] = c_grp
-            copy = nc.vector.tensor_copy if (cp, v) in c_on_vector else nc.scalar.copy
-            copy(
-                out=c_grp[:].bitcast(F32),
-                in_=c_banks.pop((cp, v))[:].rearrange("p u c -> p c u"),
-            )
+            copy = nc.scalar.copy if on_scalar else nc.vector.tensor_copy
+            copy(out=c_grp[:].bitcast(F32), in_=c_banks.pop((cp, v))[:].rearrange("p u c -> p c u"))
 
         def quantise_c(cp, v):
-            cols = slice(2 * P * cp, 2 * P * (cp + 1))
+            cols = slice(PAIR * cp, PAIR * (cp + 1))
             nc.vector.quantize_mx(
                 out=c_words[:, v, cols].bitcast(FP8X4),
                 scales=c_scales[:, v, cols],
@@ -233,91 +300,19 @@ def tile_qccpn_pa_kernel(
             )
 
         def transpose_c2(cp):
-            c2_ps = psum.tile([P, 2 * P], F32, tag="tc", bufs=2)
+            c2_ps = psum.tile([P, PAIR], F32, tag="tc", bufs=2)
             for i in range(2):
                 column = c2_cols[:, 2 * cp + i : 2 * cp + i + 1]
                 nc.tensor.transpose(c2_ps[:, i * P : (i + 1) * P], column.to_broadcast([P, P]), ident_f32[:])
             c_banks[cp] = c2_ps
 
         def copy_c2(cp):
-            nc.vector.tensor_copy(out=c2_rows[:, 2 * P * cp : 2 * P * (cp + 1)], in_=c_banks.pop(cp)[:])
+            nc.vector.tensor_copy(out=c2_rows[:, PAIR * cp : PAIR * (cp + 1)], in_=c_banks.pop(cp)[:])
 
-        def project(u, k):
-            w = weight_of_view[units[u][1]]
-            acc = psum.tile([P, 2, ROWS], F32, tag="s1", bufs=2)
-            for i in range(2):
-                cols = slice((2 * k + i) * P, (2 * k + i + 1) * P)
-                for g in range(IN_PASSES):
-                    nc.tensor.matmul_mx(
-                        out=acc[:, i, :],
-                        lhsT=w_words[:, w, g, cols].bitcast(FP8X4),
-                        lhsT_scale=w_scales[4 * g : P, w, cols],
-                        rhs=x_operands[u][0][:, g, :].bitcast(FP8X4),
-                        rhs_scale=x_operands[u][1][:, g, :],
-                        start=(g == 0),
-                        stop=(g == IN_PASSES - 1),
-                    )
-            s1_banks[u, k] = acc
-
-        def relu(u, k):
-            w = weight_of_view[units[u][1]]
-            if k == 0:
-                feat = stream.tile([P, PACK, ROWS], F32, tag="feat", bufs=4)
-                feats[u] = feat
-            acc = s1_banks.pop((u, k))
-            for i in (1, 0):
-                nc.scalar.activation(
-                    out=feats[u][:, 2 * k + i, :], in_=acc[:, i, :], func=ACT.Relu, bias=bias_cols[:, w, k, i : i + 1]
-                )
-
-        def lay_out_feat(u):
-            f_grp = stream.tile([P, ROWS, PACK], BF16, tag="f_grp", align_bytes=64)
-            f_groups[u] = f_grp
-            nc.vector.tensor_copy(
-                out=f_grp[:].rearrange("p (b i) t -> p b t i", i=4),
-                in_=feats[u][:].rearrange("p t (b i) -> p b t i", i=4),
-            )
-
-        def quantise_feat(u):
-            h, v = units[u]
-            if v == 0:
-                f_words = stream.tile([P, VIEWS, ROWS], U32, tag="f_words", bufs=CHUNKS, align_bytes=64)
-                f_scales = stream.tile([P, VIEWS, ROWS], U8, tag="f_scales", bufs=CHUNKS, align_bytes=64)
-                f_operands[h] = (f_words, f_scales)
-            f_words, f_scales = f_operands[h]
-            nc.vector.quantize_mx(
-                out=f_words[:, v, :].bitcast(FP8X4),
-                scales=f_scales[:, v, :],
-                in_=f_groups.pop(u)[:].rearrange("p b t -> p (b t)"),
-            )
-
-        def transpose_feat(u, j):
-            ft = psum.tile([P, BANK], F32, tag="tf", bufs=2)
-            for t in range(PACK):
-                nc.tensor.transpose(ft[:, t * P : (t + 1) * P], feats[u][:, t, j * P : (j + 1) * P], ident_f32[:])
-            f_banks[u, j] = ft
-
-        def square_feat(u, j):
-            h, v = units[u]
-            f_sq = stream.tile([P, BANK], BF16, tag="f_sq")
-            nc.scalar.activation(
-                out=f_sq[:],
-                in_=f_banks.pop((u, j))[:],
-                func=ACT.Square,
-                scale=math.sqrt(0.5),
-                accum_out=f2_parts[:, ROW_TILES * h + j, v : v + 1],
-            )
-
-        def sum_f2(h):
-            rows = slice(ROW_TILES * h, ROW_TILES * (h + 1))
-            nc.vector.tensor_reduce(
-                out=f2_cols[:, rows], in_=f2_parts[:, rows, :], axis=mybir.AxisListType.X, op=ALU.add
-            )
-
-        def score(c, j, first, width):
+        def score(chunk, j, first, width):
             rows = slice(j * P, (j + 1) * P)
             cols = slice(first, first + width)
-            f_words, f_scales = f_operands[c]
+            f_words, f_scales = f_operands[chunk]
             cross = psum.tile([P, width], F32, tag="tc", bufs=2)
             for v in range(VIEWS):
                 nc.tensor.matmul_mx(
@@ -329,154 +324,142 @@ def tile_qccpn_pa_kernel(
                     start=(v == 0),
                     stop=(v == VIEWS - 1),
                 )
-            score_banks[c, j, first] = cross
+            score_banks[chunk, j, first] = cross
 
-        def take_score(c, j, first, width):
-            row = ROW_TILES * c + j
-            half = stream.tile([P, width], F32, tag="half", bufs=4)
+        def halve(chunk, j, first, width):
+            row = ROW_TILES * chunk + j
+            t = stream.tile([P, width], F32, tag="t", bufs=4)
             nc.vector.scalar_tensor_tensor(
-                out=half[:],
-                in0=score_banks.pop((c, j, first))[:],
+                out=t[:],
+                in0=score_banks.pop((chunk, j, first))[:],
                 scalar=f2_cols[:, row : row + 1],
                 in1=c2_rows[:, first : first + width],
                 op0=ALU.subtract,
                 op1=ALU.subtract,
             )
-            half_tiles[c, j, first] = half
+            half_tiles[chunk, j, first] = t
 
-        def root(c, j, first, width):
+        def root(chunk, j, first, width):
             r = stream.tile([P, width], F32, tag="r", bufs=4)
             nc.scalar.activation(
                 out=r[:],
-                in_=half_tiles[c, j, first][:],
+                in_=half_tiles[chunk, j, first][:],
                 func=ACT.Abs_reciprocal_sqrt,
                 scale=0.5 / GAMMA**2,
                 bias=tiny[:],
             )
-            root_tiles[c, j, first] = r
+            root_tiles[chunk, j, first] = r
 
-        def store(c, j, first, width):
+        def store(chunk, j, first, width):
             scores = stream.tile([P, width], F32, tag="scores", bufs=4)
             nc.vector.scalar_tensor_tensor(
                 out=scores[:],
-                in0=half_tiles.pop((c, j, first))[:],
+                in0=half_tiles.pop((chunk, j, first))[:],
                 scalar=0.0,
-                in1=root_tiles.pop((c, j, first))[:],
+                in1=root_tiles.pop((chunk, j, first))[:],
                 op0=ALU.min,
                 op1=ALU.mult,
             )
-            out_rows = out.rearrange("(h p j) c -> h j p c", h=CHUNKS, p=P)
-            nc.sync.dma_start(out=out_rows[c, j][:, first : first + width], in_=scores[:])
+            out_rows = out.rearrange("(c p j) k -> c j p k", c=CHUNKS, p=P)
+            nc.sync.dma_start(out=out_rows[chunk, j][:, first : first + width], in_=scores[:])
 
         def part_of(step, lag):
             k = step - lag
             return divmod(k, PARTS) if 0 <= k < UNITS * PARTS else None
 
-        last_split = 2
-        doubled_from = 16
-        tail = 37
-        c_on_vector = [(a, b) for a in range(4) for b in (0, 1, 2)]
-        w_steps = (4, 5)
-        score_at = [20, 22, 24, 26, 29, 30, 31, 32, 33, 34, 36, 37, 38, 39, 40, 41]
-        x_on_scalar = [(0, 1), (1, 1)] + [(u, 0) for u in range(3, 16, 4)]
-        centre_at = [4, 5, 6, 7] + list(range(8, 12)) + list(range(12, 28, 2))
-        square_at = [3, 4, 5, 6] + list(range(7, 11)) + list(range(11, 27, 2))
-        centre_jobs = {}
-        for k, s in enumerate(centre_at):
-            centre_jobs.setdefault(s, []).append(divmod(k, VIEWS))
-        square_jobs, c2_steps, sum2_steps = {}, {}, {}
-        for k, sq in enumerate(square_at):
-            square_jobs.setdefault(sq, []).append(divmod(k, 2))
-            if k % 4 == 3:
-                sum2_steps[sq + 1] = k // 4
-                c2_steps[sq + 3] = k // 4
-        score_order = []
-        for c, ch in ((0, 0), (1, 0), (0, 1), (1, 1), (2, 0), (2, 1), (3, 0), (3, 1)):
+        centre_at, square_at, sum_c2_at, spread_c2_at = {}, {}, {}, {}
+        for k in range(CENTRE_JOBS):
+            step = 4 + k if k < 2 * VIEWS else 12 + 2 * (k - 2 * VIEWS)
+            centre_at[step] = divmod(k, VIEWS)
+            square_at[step - 1] = divmod(k, 2)
+            if k % VIEWS == VIEWS - 1:
+                sum_c2_at[step] = k // VIEWS
+                spread_c2_at[step + 2] = k // VIEWS
+
+        order = [(0, 0), (1, 0), (0, 1), (1, 1), (2, 0), (2, 1), (3, 0), (3, 1)]
+        groups = [(chunk, j, BANK * ch, BANK) for chunk, ch in order for j in range(ROW_TILES)]
+        score_at, root_at, store_at = {}, {}, {}
+        for n, group in enumerate(groups):
+            step = 20 + 2 * n if n < 5 else 26 + n
+            parts = [group]
+            if n == len(groups) - 1:
+                chunk, j, first, width = group
+                parts = [(chunk, j, first, width // 2), (chunk, j, first + width // 2, width // 2)]
+            wait = 1 if step < X_STEPS else 0
+            score_at[step] = parts
+            root_at[step + 1 + wait] = root_at.get(step + 1 + wait, []) + parts
+            store_at[step + 2 + wait] = store_at.get(step + 2 + wait, []) + parts
+        first_score, last_step = min(score_at), max(store_at)
+
+        norm_at, sum_f2_at = {}, {}
+        for u, (chunk, v) in enumerate(units):
             for j in range(ROW_TILES):
-                score_order.append([(c, j, BANK * ch, BANK)])
-        c, j, first, width = score_order[-1][0]
-        score_order[-1] = [(c, j, first + k * width // last_split, width // last_split) for k in range(last_split)]
-        score_steps = {}
-        for s, group in zip(score_at, score_order):
-            score_steps.setdefault(s, []).extend(group)
-        norm_steps, sum_steps = {}, {}
-        for u in range(UNITS):
-            for j in range(ROW_TILES):
-                s = PARTS * u + NORM_LAG + (j if u < UNITS - 1 else 0)
-                norm_steps.setdefault(s, []).append((u, j))
-                if units[u][1] == VIEWS - 1 and j == ROW_TILES - 1:
-                    sum_steps[s + 1] = units[u][0]
-        summed = {c: s for s, c in sum_steps.items()}
-        take_steps, root_steps, store_steps = {}, {}, {}
-        for s, group in zip(score_at, score_order):
-            f = max(s + 1, summed[group[0][0]])
-            take_steps.setdefault(f, []).extend(group)
-            root_steps.setdefault(f + (0 if s >= tail else 1), []).extend(group)
-            store_steps.setdefault(f + (1 if s >= tail else 2), []).extend(group)
+                step = PARTS * u + FEAT_LAG + (j if u < UNITS - 1 else 0)
+                norm_at[step] = norm_at.get(step, []) + [(u, j)]
+            if v == VIEWS - 1:
+                sum_f2_at[step + 1] = chunk
 
         def transposes(step):
-            for norm in norm_steps.get(step, []):
+            for norm in norm_at.get(step, []):
                 transpose_feat(*norm)
-            xs = part_of(step, START)
-            if xs:
-                transpose_x(*xs)
-            for job in centre_jobs.get(step, []):
-                transpose_c(*job)
-            if step in c2_steps:
-                transpose_c2(c2_steps[step])
+            x_part = part_of(step, 0)
+            if x_part:
+                transpose_x(*x_part)
+            if step in centre_at:
+                transpose_c(*centre_at[step])
+            if step in spread_c2_at:
+                transpose_c2(spread_c2_at[step])
 
         transposes(0)
-        for step in range(60):
-            xs = part_of(step, START)
-            rel = part_of(step, RELU_LAG)
-            if rel:
-                relu(*rel)
-            fq = part_of(step, FEAT_QUANT_LAG)
-            if fq and fq[1] == 0:
-                quantise_feat(fq[0])
-            if step in sum_steps:
-                sum_f2(sum_steps[step])
-            for group in take_steps.get(step, []):
-                take_score(*group)
-            for job in centre_jobs.get(step, []):
-                copy_c(*job)
-            if xs:
-                copy_x(*xs)
-            for norm in norm_steps.get(step, []):
+        for step in range(last_step + 1):
+            relu_part = part_of(step, RELU_LAG)
+            if relu_part:
+                relu(*relu_part)
+            feat_part = part_of(step, FEAT_LAG)
+            if feat_part and feat_part[1] == 0:
+                quantise_feat(feat_part[0])
+            if step in centre_at:
+                copy_c(*centre_at[step])
+            x_part = part_of(step, 0)
+            if x_part:
+                copy_x(*x_part)
+            if step in sum_f2_at:
+                sum_f2(sum_f2_at[step])
+            for group in score_at.get(step - 1, []):
+                halve(*group)
+            for norm in norm_at.get(step, []):
                 square_feat(*norm)
-            if step in c2_steps:
-                copy_c2(c2_steps[step])
-            xq = part_of(step, QUANT_LAG)
-            if xq and xq[1] == 0:
-                quantise_x(xq[0])
-            for job in centre_jobs.get(step - 1, []):
-                quantise_c(*job)
-            if step == w_steps[0]:
-                permute_weight(0, 0)
-                permute_weight(0, 1)
+            if step in spread_c2_at:
+                copy_c2(spread_c2_at[step])
+            quant_part = part_of(step, QUANT_LAG)
+            if quant_part and quant_part[1] == 0:
+                quantise_x(quant_part[0])
+            if step - 1 in centre_at:
+                quantise_c(*centre_at[step - 1])
+            if step == 4:
+                permute_weight(0)
                 spread_bias()
-            if step == w_steps[1]:
-                permute_weight(1, 0)
-                permute_weight(1, 1)
-            for job in square_jobs.get(step, []):
-                square_c(*job)
-            if step in sum2_steps:
-                sum_c2(sum2_steps[step])
-            for group in root_steps.get(step, []):
+            if step == 5:
+                permute_weight(1)
+            if step in square_at:
+                square_c(*square_at[step])
+            if step in sum_c2_at:
+                sum_c2(sum_c2_at[step])
+            for group in root_at.get(step, []):
                 root(*group)
-            lay = part_of(step, LAYOUT_LAG)
-            if lay and lay[1] == 0:
-                lay_out_feat(lay[0])
-            for group in store_steps.get(step, []):
+            layout_part = part_of(step, LAYOUT_LAG)
+            if layout_part and layout_part[1] == 0:
+                lay_out_feat(layout_part[0])
+            for group in store_at.get(step, []):
                 store(*group)
 
-            early = step >= doubled_from and step % 2 == 0
-            if early:
+            together = step >= first_score and step % 2 == 0
+            if together:
                 transposes(step + 1)
-            proj = part_of(step, PROJECT_LAG)
-            if proj:
-                project(*proj)
-            for group in score_steps.get(step, []):
+            project_part = part_of(step, PROJECT_LAG)
+            if project_part:
+                project(*project_part)
+            for group in score_at.get(step, []):
                 score(*group)
-            if not early:
+            if not together:
                 transposes(step + 1)

@@ -30,6 +30,7 @@ UNITS = CHUNKS * VIEWS
 PARTS = 2
 PAIR = 2 * P
 CENTRE_PAIRS = NCLASS // PAIR
+CENTRE_TILES = BANK // P
 CENTRE_JOBS = CENTRE_PAIRS * VIEWS
 
 QUANT_LAG = 2
@@ -108,11 +109,11 @@ def tile_qccpn_pa_kernel(
                 nc.sync.dma_start(out=bias_rows[2 * w : 2 * w + 2, :], in_=bias.rearrange("(u m) -> u m", u=2))
 
         load_x(pieces=2)
+        load_biases()
         load_x()
         load_x()
         load_centres()
         load_weight(0)
-        load_biases()
         load_x()
         load_weight(1)
         for i in range(CENTRE_PAIRS - 1):
@@ -293,21 +294,22 @@ def tile_qccpn_pa_kernel(
                 accum_out=c2_parts[:, i, half : half + 1],
             )
 
-        def sum_c2(cp):
-            tiles = slice(2 * cp, 2 * cp + 2)
+        def sum_c2(ch):
+            tiles = slice(CENTRE_TILES * ch, CENTRE_TILES * (ch + 1))
             nc.vector.tensor_reduce(
                 out=c2_cols[:, tiles], in_=c2_parts[:, tiles, :], axis=mybir.AxisListType.X, op=ALU.add
             )
 
-        def transpose_c2(cp):
-            c2_ps = psum.tile([P, PAIR], F32, tag="tc", bufs=2)
-            for i in range(2):
-                column = c2_cols[:, 2 * cp + i : 2 * cp + i + 1]
-                nc.tensor.transpose(c2_ps[:, i * P : (i + 1) * P], column.to_broadcast([P, P]), ident_f32[:])
-            c_banks[cp] = c2_ps
+        def transpose_c2(ch):
+            c2_ps = psum.tile([P, BANK], F32, tag="tc", bufs=2)
+            for i in range(CENTRE_TILES):
+                tile = CENTRE_TILES * ch + i
+                column = c2_cols[:, tile : tile + 1].to_broadcast([P, P])
+                nc.tensor.transpose(c2_ps[:, i * P : (i + 1) * P], column, ident_f32[:])
+            c_banks[ch] = c2_ps
 
-        def copy_c2(cp):
-            nc.vector.tensor_copy(out=c2_rows[:, PAIR * cp : PAIR * (cp + 1)], in_=c_banks.pop(cp)[:])
+        def copy_c2(ch):
+            nc.vector.tensor_copy(out=c2_rows[:, BANK * ch : BANK * (ch + 1)], in_=c_banks.pop(ch)[:])
 
         def score(chunk, j, first, width):
             rows = slice(j * P, (j + 1) * P)
@@ -372,9 +374,9 @@ def tile_qccpn_pa_kernel(
             step = 4 + k if k < 2 * VIEWS else 12 + 2 * (k - 2 * VIEWS)
             centre_at[step] = divmod(k, VIEWS)
             square_at[step - 1] = divmod(k, 2)
-            if k % VIEWS == VIEWS - 1:
-                sum_c2_at[step] = k // VIEWS
-                spread_c2_at[step + 2] = k // VIEWS
+            if k % (2 * VIEWS) == 2 * VIEWS - 1:
+                sum_c2_at[step] = k // (2 * VIEWS)
+                spread_c2_at[step + 2] = k // (2 * VIEWS)
 
         order = [(0, 0), (1, 0), (0, 1), (1, 1), (2, 0), (2, 1), (3, 0), (3, 1)]
         groups = [(chunk, j, BANK * ch, BANK) for chunk, ch in order for j in range(ROW_TILES)]
@@ -436,9 +438,10 @@ def tile_qccpn_pa_kernel(
                 quantise_x(quant_part[0])
             if step - 1 in centre_at:
                 quantise_c(*centre_at[step - 1])
+            if step == 3:
+                spread_bias()
             if step == 4:
                 permute_weight(0)
-                spread_bias()
             if step == 5:
                 permute_weight(1)
             if step in square_at:

import math
from contextlib import ExitStack

import concourse.mybir as mybir
from concourse.masks import make_identity

F32 = mybir.dt.float32
BF16 = mybir.dt.bfloat16
I32 = mybir.dt.int32
U32 = mybir.dt.uint32
U8 = mybir.dt.uint8
FP8X4 = mybir.dt.float8_e4m3fn_x4
ACT = mybir.ActivationFunctionType
ALU = mybir.AluOpType

P = 128
PACK = 4
BANK = 512

BATCH, IN_F, FEAT, NCLASS = 1024, 1024, 512, 1024
VIEWS = 4
D = VIEWS * FEAT
GAMMA = 0.1

IN_PASSES = IN_F // (P * PACK)
ROWS = 256
CHUNKS = BATCH // ROWS
ROW_TILES = ROWS // P
UNITS = CHUNKS * VIEWS
PARTS = 2
PAIR = 2 * P
CENTRE_PAIRS = NCLASS // PAIR
CENTRE_TILES = BANK // P
CENTRE_JOBS = CENTRE_PAIRS * VIEWS

QUANT_LAG = 2
PROJECT_LAG = 5
RELU_LAG = PROJECT_LAG + 1
LAYOUT_LAG = PROJECT_LAG + 2
FEAT_LAG = PROJECT_LAG + 3
X_STEPS = UNITS * PARTS

FLOPS = 2 * BATCH * IN_F * FEAT * VIEWS + 2 * BATCH * D * NCLASS


def tile_qccpn_pa_kernel(
    tc, x, x_90, x_180, x_270, W_f_words, W_f_scales, b_f, W_r_words, W_r_scales, b_r, centers, out
):
    nc = tc.nc
    views = [x, x_90, x_180, x_270]
    weights = [(W_f_words, W_f_scales), (W_r_words, W_r_scales)]
    weight_of_view = [0, 1, 1, 1]
    units = [(chunk, v) for chunk in range(CHUNKS) for v in range(VIEWS)]

    with ExitStack() as stack:
        keep = stack.enter_context(tc.tile_pool(name="keep", bufs=1))
        stream = stack.enter_context(tc.tile_pool(name="stream", bufs=2))
        psum = stack.enter_context(tc.psum_pool(name="psum", bufs=2))
        stack.enter_context(tc.manual_schedule())

        ident_f32 = keep.tile([P, P], F32)
        make_identity(nc, ident_f32[:])

        one = keep.tile([P, 1], F32)
        nc.vector.memset(one[:], 1.0)
        root_of_one = keep.tile([P, 1], F32)
        nc.scalar.activation(out=root_of_one[:], in_=one[:], func=ACT.Abs_reciprocal_sqrt)
        tiny = keep.tile([P, 1], F32)
        nc.vector.memset(tiny[:], 1e-30)

        x_tiles, c_tiles = [], []

        def load_x(pieces=1):
            chunk, v = units[len(x_tiles)]
            x_raw = stream.tile([P, ROW_TILES, IN_F], BF16, tag="x_raw", bufs=10)
            rows = views[v].rearrange("(c p j) k -> c p j k", c=CHUNKS, p=P)
            for i in range(pieces):
                cols = slice(i * IN_F // pieces, (i + 1) * IN_F // pieces)
                nc.sync.dma_start(out=x_raw[:, :, cols], in_=rows[chunk][:, :, cols])
            x_tiles.append(x_raw)

        def load_centres():
            c_raw = stream.tile([P, 2, D], BF16, tag="c_raw", bufs=CENTRE_PAIRS)
            rows = centers.rearrange("(cp i p) k -> cp i p k", cp=CENTRE_PAIRS, p=P)
            for i in range(2):
                nc.sync.dma_start(out=c_raw[:, i, :], in_=rows[len(c_tiles), i])
            c_tiles.append(c_raw)

        w_raw = [keep.tile([P, IN_PASSES, FEAT], U32, align_bytes=64, name="w_raw%d" % w) for w in range(2)]
        s_raw = [keep.tile([P, FEAT], U8, align_bytes=64, name="s_raw%d" % w) for w in range(2)]
        bias_rows = keep.tile([P, 2 * P], BF16)
        for w in range(2):
            nc.vector.memset(s_raw[w][:].bitcast(I32), 0)
        nc.vector.memset(bias_rows[:], 0.0)

        def load_weight(w):
            words, scales = weights[w]
            nc.sync.dma_start(
                out=w_raw[w][:].bitcast(I32), in_=words.rearrange("g p n t -> p g (n t)").bitcast(I32)
            )
            for quadrant in range(4):
                nc.sync.dma_start(
                    out=s_raw[w][32 * quadrant : 32 * quadrant + 4 * IN_PASSES, :].bitcast(I32),
                    in_=scales[:, 4 * quadrant : 4 * quadrant + 4, :].bitcast(I32),
                )

        def load_biases():
            for w, bias in enumerate((b_f, b_r)):
                nc.sync.dma_start(out=bias_rows[2 * w : 2 * w + 2, :], in_=bias.rearrange("(u m) -> u m", u=2))

        load_x(pieces=2)
        load_biases()
        load_x()
        load_x()
        load_centres()
        load_weight(0)
        load_x()
        load_weight(1)
        for i in range(CENTRE_PAIRS - 1):
            load_centres()
            load_x()
        for u in range(len(x_tiles), UNITS):
            load_x()

        w_words = keep.tile([P, 2, IN_PASSES, FEAT], U32, align_bytes=64)
        w_scales = keep.tile([P, 2, FEAT], U8, align_bytes=64)
        bias_cols = keep.tile([P, 2, 2, 2], F32)

        c_words = keep.tile([P, VIEWS, NCLASS], U32, align_bytes=64)
        c_scales = keep.tile([P, VIEWS, NCLASS], U8, align_bytes=64)
        c2_parts = keep.tile([P, NCLASS // P, 2], F32)
        c2_cols = keep.tile([P, NCLASS // P], F32)
        c2_rows = keep.tile([P, NCLASS], F32)
        f2_parts = keep.tile([P, CHUNKS * ROW_TILES, VIEWS], F32)
        f2_cols = keep.tile([P, CHUNKS * ROW_TILES], F32)

        x_banks, x_groups, x_operands = {}, {}, {}
        c_banks, c_groups = {}, {}
        feat_banks, feats, f_groups, f_banks, f_operands = {}, {}, {}, {}, {}
        score_banks, half_tiles, root_tiles = {}, {}, {}

        def permute_weight(w):
            for u in range(2):
                cols = slice(2 * P * u, 2 * P * (u + 1))
                nc.vector.tensor_copy(
                    out=w_words[:, w, :, cols].bitcast(I32).rearrange("p g (e m) -> p g e m", e=2),
                    in_=w_raw[w][:, :, cols].bitcast(I32).rearrange("p g (m e) -> p g e m", e=2),
                )
                nc.vector.tensor_copy(
                    out=w_scales[:, w, cols].rearrange("p (e m) -> p e m", e=2),
                    in_=s_raw[w][:, cols].rearrange("p (m e) -> p e m", e=2),
                )

        def spread_bias():
            bias_ps = psum.tile([P, P], F32, tag="tc", bufs=2)
            nc.tensor.transpose(bias_ps[:], bias_rows[:].bitcast(F32), ident_f32[:])
            nc.vector.tensor_copy(
                out=bias_cols[:].rearrange("p w u e -> p (w u e)"), in_=bias_ps[:].bitcast(BF16)[:, 0:8]
            )

        def transpose_x(u, g):
            xt = psum.tile([P, 2, ROWS], F32, tag="tx", bufs=2)
            for j in range(ROW_TILES):
                words = x_tiles[u][:, j, :].bitcast(F32)
                for e in range(2):
                    nc.tensor.transpose(
                        xt[:, e, j * P : (j + 1) * P], words[:, 256 * g + e : 256 * (g + 1) : 2], ident_f32[:]
                    )
            x_banks[u, g] = xt

        def copy_x(u, g):
            if g == 0:
                x_grp = stream.tile([P, IN_PASSES, ROWS, PACK], BF16, tag="x_grp", bufs=3, align_bytes=64)
                x_groups[u] = x_grp
            on_scalar = (g == 1 and u < 2) or (g == 0 and u % 4 == 3)
            copy = nc.scalar.copy if on_scalar else nc.vector.tensor_copy
            copy(out=x_groups[u][:, g, :, :].bitcast(F32), in_=x_banks.pop((u, g))[:].rearrange("p e b -> p b e"))

        def quantise_x(u):
            x_words = stream.tile([P, IN_PASSES, ROWS], U32, tag="x_words", bufs=3, align_bytes=64)
            x_scales = stream.tile([P, IN_PASSES, ROWS], U8, tag="x_scales", bufs=3, align_bytes=64)
            x_operands[u] = (x_words, x_scales)
            nc.vector.quantize_mx(
                out=x_words[:].rearrange("p g b -> p (g b)").bitcast(FP8X4),
                scales=x_scales[:].rearrange("p g b -> p (g b)"),
                in_=x_groups.pop(u)[:].rearrange("p g b t -> p (g b t)"),
            )

        def project(u, k):
            w = weight_of_view[units[u][1]]
            x_words, x_scales = x_operands[u]
            acc = psum.tile([P, 2, ROWS], F32, tag="s1", bufs=2)
            for i in range(2):
                cols = slice((2 * k + i) * P, (2 * k + i + 1) * P)
                for g in range(IN_PASSES):
                    nc.tensor.matmul_mx(
                        out=acc[:, i, :],
                        lhsT=w_words[:, w, g, cols].bitcast(FP8X4),
                        lhsT_scale=w_scales[4 * g : P, w, cols],
                        rhs=x_words[:, g, :].bitcast(FP8X4),
                        rhs_scale=x_scales[:, g, :],
                        start=(g == 0),
                        stop=(g == IN_PASSES - 1),
                    )
            feat_banks[u, k] = acc

        def relu(u, k):
            w = weight_of_view[units[u][1]]
            if k == 0:
                feat = stream.tile([P, PACK, ROWS], F32, tag="feat", bufs=4)
                feats[u] = feat
            acc = feat_banks.pop((u, k))
            for i in (1, 0):
                nc.scalar.activation(
                    out=feats[u][:, 2 * k + i, :], in_=acc[:, i, :], func=ACT.Relu, bias=bias_cols[:, w, k, i : i + 1]
                )

        def lay_out_feat(u):
            f_grp = stream.tile([P, ROWS, PACK], BF16, tag="f_grp", align_bytes=64)
            f_groups[u] = f_grp
            nc.vector.tensor_copy(
                out=f_grp[:].rearrange("p (b i) t -> p b t i", i=4),
                in_=feats[u][:].rearrange("p t (b i) -> p b t i", i=4),
            )

        def quantise_feat(u):
            chunk, v = units[u]
            if v == 0:
                f_words = stream.tile([P, VIEWS, ROWS], U32, tag="f_words", bufs=CHUNKS, align_bytes=64)
                f_scales = stream.tile([P, VIEWS, ROWS], U8, tag="f_scales", bufs=CHUNKS, align_bytes=64)
                f_operands[chunk] = (f_words, f_scales)
            f_words, f_scales = f_operands[chunk]
            nc.vector.quantize_mx(
                out=f_words[:, v, :].bitcast(FP8X4),
                scales=f_scales[:, v, :],
                in_=f_groups.pop(u)[:].rearrange("p b t -> p (b t)"),
            )

        def transpose_feat(u, j):
            ft = psum.tile([P, BANK], F32, tag="tf", bufs=2)
            for t in range(PACK):
                nc.tensor.transpose(ft[:, t * P : (t + 1) * P], feats[u][:, t, j * P : (j + 1) * P], ident_f32[:])
            f_banks[u, j] = ft

        def square_feat(u, j):
            chunk, v = units[u]
            f_sq = stream.tile([P, BANK], BF16, tag="f_sq")
            nc.scalar.activation(
                out=f_sq[:],
                in_=f_banks.pop((u, j))[:],
                func=ACT.Square,
                scale=math.sqrt(0.5),
                accum_out=f2_parts[:, ROW_TILES * chunk + j, v : v + 1],
            )

        def sum_f2(chunk):
            rows = slice(ROW_TILES * chunk, ROW_TILES * (chunk + 1))
            nc.vector.tensor_reduce(
                out=f2_cols[:, rows], in_=f2_parts[:, rows, :], axis=mybir.AxisListType.X, op=ALU.add
            )

        def transpose_c(cp, v):
            ct = psum.tile([P, 2, PAIR], F32, tag="tc", bufs=2)
            for i in range(2):
                words = c_tiles[cp][:, i, :].bitcast(F32)
                for u in range(2):
                    first = 256 * v + P * u
                    nc.tensor.transpose(ct[:, u, i * P : (i + 1) * P], words[:, first : first + P], ident_f32[:])
            c_banks[cp, v] = ct

        def copy_c(cp, v):
            job = VIEWS * cp + v
            on_scalar = job < 2 * VIEWS and job % 3 == 0
            c_grp = stream.tile([P, PAIR, PACK], BF16, tag="c_grp", bufs=3, align_bytes=64)
            c_groups[cp, v] = c_grp
            copy = nc.scalar.copy if on_scalar else nc.vector.tensor_copy
            copy(out=c_grp[:].bitcast(F32), in_=c_banks.pop((cp, v))[:].rearrange("p u c -> p c u"))

        def quantise_c(cp, v):
            cols = slice(PAIR * cp, PAIR * (cp + 1))
            nc.vector.quantize_mx(
                out=c_words[:, v, cols].bitcast(FP8X4),
                scales=c_scales[:, v, cols],
                in_=c_groups.pop((cp, v))[:].rearrange("p c t -> p (c t)"),
            )

        def square_c(i, half):
            c_sq = stream.tile([P, D // 2], BF16, tag="c_sq")
            nc.scalar.activation(
                out=c_sq[:],
                in_=c_tiles[i // 2][:, i % 2, half * (D // 2) : (half + 1) * (D // 2)],
                func=ACT.Square,
                scale=math.sqrt(0.5),
                accum_out=c2_parts[:, i, half : half + 1],
            )

        def sum_c2(ch):
            tiles = slice(CENTRE_TILES * ch, CENTRE_TILES * (ch + 1))
            nc.vector.tensor_reduce(
                out=c2_cols[:, tiles], in_=c2_parts[:, tiles, :], axis=mybir.AxisListType.X, op=ALU.add
            )

        def transpose_c2(ch):
            c2_ps = psum.tile([P, BANK], F32, tag="tc", bufs=2)
            for i in range(CENTRE_TILES):
                tile = CENTRE_TILES * ch + i
                column = c2_cols[:, tile : tile + 1].to_broadcast([P, P])
                nc.tensor.transpose(c2_ps[:, i * P : (i + 1) * P], column, ident_f32[:])
            c_banks[ch] = c2_ps

        def copy_c2(ch):
            nc.vector.tensor_copy(out=c2_rows[:, BANK * ch : BANK * (ch + 1)], in_=c_banks.pop(ch)[:])

        def score(chunk, j, first, width):
            rows = slice(j * P, (j + 1) * P)
            cols = slice(first, first + width)
            f_words, f_scales = f_operands[chunk]
            cross = psum.tile([P, width], F32, tag="tc", bufs=2)
            for v in range(VIEWS):
                nc.tensor.matmul_mx(
                    out=cross[:],
                    lhsT=f_words[:, v, rows].bitcast(FP8X4),
                    lhsT_scale=f_scales[:, v, rows],
                    rhs=c_words[:, v, cols].bitcast(FP8X4),
                    rhs_scale=c_scales[:, v, cols],
                    start=(v == 0),
                    stop=(v == VIEWS - 1),
                )
            score_banks[chunk, j, first] = cross

        def halve(chunk, j, first, width):
            row = ROW_TILES * chunk + j
            t = stream.tile([P, width], F32, tag="t", bufs=4)
            nc.vector.scalar_tensor_tensor(
                out=t[:],
                in0=score_banks.pop((chunk, j, first))[:],
                scalar=f2_cols[:, row : row + 1],
                in1=c2_rows[:, first : first + width],
                op0=ALU.subtract,
                op1=ALU.subtract,
            )
            half_tiles[chunk, j, first] = t

        def root(chunk, j, first, width):
            r = stream.tile([P, width], F32, tag="r", bufs=4)
            nc.scalar.activation(
                out=r[:],
                in_=half_tiles[chunk, j, first][:],
                func=ACT.Abs_reciprocal_sqrt,
                scale=0.5 / GAMMA**2,
                bias=tiny[:],
            )
            root_tiles[chunk, j, first] = r

        def store(chunk, j, first, width):
            scores = stream.tile([P, width], F32, tag="scores", bufs=4)
            nc.vector.scalar_tensor_tensor(
                out=scores[:],
                in0=half_tiles.pop((chunk, j, first))[:],
                scalar=0.0,
                in1=root_tiles.pop((chunk, j, first))[:],
                op0=ALU.min,
                op1=ALU.mult,
            )
            out_rows = out.rearrange("(c p j) k -> c j p k", c=CHUNKS, p=P)
            nc.sync.dma_start(out=out_rows[chunk, j][:, first : first + width], in_=scores[:])

        def part_of(step, lag):
            k = step - lag
            return divmod(k, PARTS) if 0 <= k < UNITS * PARTS else None

        centre_at, square_at, sum_c2_at, spread_c2_at = {}, {}, {}, {}
        for k in range(CENTRE_JOBS):
            step = 4 + k if k < 2 * VIEWS else 12 + 2 * (k - 2 * VIEWS)
            centre_at[step] = divmod(k, VIEWS)
            square_at[step - 1] = divmod(k, 2)
            if k % (2 * VIEWS) == 2 * VIEWS - 1:
                sum_c2_at[step] = k // (2 * VIEWS)
                spread_c2_at[step + 2] = k // (2 * VIEWS)

        order = [(0, 0), (1, 0), (0, 1), (1, 1), (2, 0), (2, 1), (3, 0), (3, 1)]
        groups = [(chunk, j, BANK * ch, BANK) for chunk, ch in order for j in range(ROW_TILES)]
        score_at, root_at, store_at = {}, {}, {}
        for n, group in enumerate(groups):
            step = 20 + 2 * n if n < 5 else 26 + n
            parts = [group]
            if n == len(groups) - 1:
                chunk, j, first, width = group
                parts = [(chunk, j, first, width // 2), (chunk, j, first + width // 2, width // 2)]
            wait = 1 if step < X_STEPS else 0
            score_at[step] = parts
            root_at[step + 1 + wait] = root_at.get(step + 1 + wait, []) + parts
            store_at[step + 2 + wait] = store_at.get(step + 2 + wait, []) + parts
        first_score, last_step = min(score_at), max(store_at)

        norm_at, sum_f2_at = {}, {}
        for u, (chunk, v) in enumerate(units):
            for j in range(ROW_TILES):
                step = PARTS * u + FEAT_LAG + (j if u < UNITS - 1 else 0)
                norm_at[step] = norm_at.get(step, []) + [(u, j)]
            if v == VIEWS - 1:
                sum_f2_at[step + 1] = chunk

        def transposes(step):
            for norm in norm_at.get(step, []):
                transpose_feat(*norm)
            x_part = part_of(step, 0)
            if x_part:
                transpose_x(*x_part)
            if step in centre_at:
                transpose_c(*centre_at[step])
            if step in spread_c2_at:
                transpose_c2(spread_c2_at[step])

        transposes(0)
        for step in range(last_step + 1):
            relu_part = part_of(step, RELU_LAG)
            if relu_part:
                relu(*relu_part)
            feat_part = part_of(step, FEAT_LAG)
            if feat_part and feat_part[1] == 0:
                quantise_feat(feat_part[0])
            if step in centre_at:
                copy_c(*centre_at[step])
            x_part = part_of(step, 0)
            if x_part:
                copy_x(*x_part)
            if step in sum_f2_at:
                sum_f2(sum_f2_at[step])
            for group in score_at.get(step - 1, []):
                halve(*group)
            for norm in norm_at.get(step, []):
                square_feat(*norm)
            if step in spread_c2_at:
                copy_c2(spread_c2_at[step])
            quant_part = part_of(step, QUANT_LAG)
            if quant_part and quant_part[1] == 0:
                quantise_x(quant_part[0])
            if step - 1 in centre_at:
                quantise_c(*centre_at[step - 1])
            if step == 3:
                spread_bias()
            if step == 4:
                permute_weight(0)
            if step == 5:
                permute_weight(1)
            if step in square_at:
                square_c(*square_at[step])
            if step in sum_c2_at:
                sum_c2(sum_c2_at[step])
            for group in root_at.get(step, []):
                root(*group)
            layout_part = part_of(step, LAYOUT_LAG)
            if layout_part and layout_part[1] == 0:
                lay_out_feat(layout_part[0])
            for group in store_at.get(step, []):
                store(*group)

            together = step >= first_score and step % 2 == 0
            if together:
                transposes(step + 1)
            project_part = part_of(step, PROJECT_LAG)
            if project_part:
                project(*project_part)
            for group in score_at.get(step, []):
                score(*group)
            if not together:
                transposes(step + 1)
